import numpy as np
import ml_dtypes


def mxq(x, axis, fmt="e4m3"):
    dtype, down = {"e4m3": (ml_dtypes.float8_e4m3fn, 7), "e5m2": (ml_dtypes.float8_e5m2, 14)}[fmt]
    v = np.moveaxis(np.asarray(x, np.float32).astype(ml_dtypes.bfloat16).astype(np.float64), axis, -1)
    blocks = v.reshape(v.shape[:-1] + (-1, 32))
    amax = np.abs(blocks).max(-1, keepdims=True)
    byte = np.maximum(np.where(amax > 0, np.frexp(amax)[1] - 1 + 127, 0) - down, 1)
    scale = np.exp2(byte - 127.0)
    codes = (blocks / scale).astype(np.float32).astype(dtype).astype(np.float64)
    return np.moveaxis((codes * scale).reshape(v.shape), -1, axis)


WIDE = False


def mx_kscale(k):
    if not WIDE:
        return np.ones(k)
    levels = np.array([10, -10, 5, -5, 0])
    a = np.random.permutation(np.resize(levels, k // 512 * 4)).reshape(k // 512, 4)
    idx = np.arange(k)
    return np.exp2(a[idx // 512, idx % 128 // 32])


BF16 = ml_dtypes.bfloat16


def bf(x):
    return np.asarray(x, np.float32).astype(BF16)


def f64(x):
    return np.asarray(x).astype(np.float64)


B, S, D, H, KVH, DH, F = 2, 2048, 512, 8, 2, 128, 512
EPS = 1e-6
E = H * DH


def rms_norm(v, eps):
    return v / np.sqrt(np.mean(np.square(v), axis=-1, keepdims=True) + eps)


def setup_inputs():
    s = mx_kscale(E)
    return {"y_attn": bf(np.random.standard_normal((B, H, S, DH)) * 0.35 * s.reshape(H, 1, DH)),
            "x": bf(np.random.standard_normal((B, S, D))),
            "w_o": bf(np.random.standard_normal((D, E)) / np.sqrt(E) / s[None, :]),
            "attn_scale": bf(1.0 + 0.1 * np.random.standard_normal(D)),
            "w_fc": bf(np.random.standard_normal((F, D)) / np.sqrt(D))}


def reference(y_attn, x, w_o, attn_scale, w_fc):
    yc = f64(y_attn).transpose(0, 2, 1, 3).reshape(B, S, E)
    attn_out = mxq(yc, 2, "e4m3") @ mxq(f64(w_o), 1, "e4m3").T
    x_mid = f64(x) + f64(attn_scale)[None, None, :] * attn_out
    h = mxq(rms_norm(x_mid, EPS), 2, "e4m3") @ mxq(f64(w_fc), 1, "e4m3").T
    h = np.square(np.maximum(h, 0.0))
    return x_mid, h

@@ -1,0 +1,318 @@
+from contextlib import ExitStack
+
+import concourse.mybir as mybir
+from concourse.masks import make_identity
+
+BF16 = mybir.dt.bfloat16
+F32 = mybir.dt.float32
+U32 = mybir.dt.uint32
+U8 = mybir.dt.uint8
+FP8X4 = mybir.dt.float8_e4m3fn_x4
+ALU = mybir.AluOpType
+ACT = mybir.ActivationFunctionType
+
+P = 128
+PACK = 4
+K_PASS = P * PACK
+
+B, H, S, DH = 2, 8, 2048, 128
+E = H * DH
+D = 512
+F = 512
+EPS = 1e-6
+
+PASSES_1 = E // K_PASS
+TILES_PER_CHUNK = 8
+CHUNK_TOKENS = P * TILES_PER_CHUNK
+CHUNKS_PER_BATCH = S // CHUNK_TOKENS
+N_CHUNKS = B * CHUNKS_PER_BATCH
+N_TILES = N_CHUNKS * TILES_PER_CHUNK
+TILES_PER_STORE = 2
+N_STAGES = 13
+
+FLOPS = 2 * B * S * E * D + 2 * B * S * D * F
+
+
+def transpose_pairs(nc, bank, rows, identity_f32):
+    words = rows.bitcast(F32)
+    for q in range(E // (2 * P)):
+        nc.tensor.transpose(bank[:, q, :], words[:, q * P : (q + 1) * P], identity_f32)
+
+
+def transpose_singles(nc, bank, rows, identity_bf16):
+    for t in range(PACK):
+        nc.tensor.transpose(bank[:, t, :], rows[:, t * P : (t + 1) * P], identity_bf16)
+
+
+def pairs_side_by_side(bank):
+    return bank.rearrange("p (g u) r -> p g r u", u=2)
+
+
+def singles_side_by_side(bank):
+    return bank.rearrange("p t r -> p r t")
+
+
+def tile_shepherdembryo_pb_t_kernel(tc, y_attn, x, w_o, attn_scale, w_fc, out_0, out_1):
+    nc = tc.nc
+
+    def token_rows(dram, chunk):
+        b, part = divmod(chunk, CHUNKS_PER_BATCH)
+        rows = dram[b, part * CHUNK_TOKENS : (part + 1) * CHUNK_TOKENS, :]
+        return rows.rearrange("(p i) d -> p i d", i=TILES_PER_CHUNK)
+
+    with ExitStack() as stack:
+        stack.enter_context(tc.manual_schedule())
+        const = stack.enter_context(tc.tile_pool(name="const", bufs=1))
+        resident = stack.enter_context(tc.tile_pool(name="resident", bufs=N_CHUNKS))
+        work = stack.enter_context(tc.tile_pool(name="work", bufs=3))
+        results = stack.enter_context(tc.tile_pool(name="results", bufs=4))
+        psum = stack.enter_context(tc.psum_pool(name="psum", bufs=2))
+
+        identity_f32 = const.tile([P, P], F32)
+        make_identity(nc, identity_f32[:])
+        identity_bf16 = const.tile([P, P], BF16)
+        make_identity(nc, identity_bf16[:])
+        ones = const.tile([P, P], BF16)
+        nc.vector.memset(ones[:], 1.0)
+        eps = const.tile([P, 1], F32)
+        nc.vector.memset(eps[:], EPS)
+        gain_rows = const.tile([P, D], BF16)
+        nc.vector.memset(gain_rows[:], 0.0)
+
+        wo_rows = const.tile([P, D // P, E], BF16)
+        nc.sync.dma_start(out=wo_rows[:], in_=w_o.rearrange("(a p) k -> p a k", p=P))
+        wfc_rows = const.tile([P, F // P, D], BF16)
+        nc.sync.dma_start(out=wfc_rows[:], in_=w_fc.rearrange("(a p) k -> p a k", p=P))
+        nc.sync.dma_start(out=gain_rows[0:1, :], in_=attn_scale.rearrange("(o d) -> o d", o=1))
+        y_chunks = []
+        x_chunks = []
+        for chunk in range(N_CHUNKS):
+            b, part = divmod(chunk, CHUNKS_PER_BATCH)
+            y_chunk = resident.tile([P, H, TILES_PER_CHUNK, DH], BF16)
+            nc.sync.dma_start(
+                out=y_chunk[:],
+                in_=y_attn[b, :, part * CHUNK_TOKENS : (part + 1) * CHUNK_TOKENS, :].rearrange(
+                    "h (p i) j -> p h i j", i=TILES_PER_CHUNK
+                ),
+            )
+            y_chunks.append(y_chunk)
+            x_chunk = resident.tile([P, TILES_PER_CHUNK, D], BF16)
+            nc.sync.dma_start(out=x_chunk[:], in_=token_rows(x, chunk))
+            x_chunks.append(x_chunk)
+
+        def copy_engine(piece):
+            return nc.scalar.copy if piece % 2 == 0 else nc.vector.tensor_copy
+
+        wo_grouped = const.tile([P, PASSES_1 * D * PACK], BF16, align_bytes=64)
+        wo_grouped_words = wo_grouped[:].bitcast(F32).rearrange("p (g r u) -> p g r u", g=PASSES_1, u=2)
+        for a in range(D // P):
+            pairs_T = psum.tile([P, PACK, P], F32)
+            transpose_pairs(nc, pairs_T, wo_rows[:, a, :], identity_f32[:])
+            copy_engine(a)(out=wo_grouped_words[:, :, a * P : (a + 1) * P, :], in_=pairs_side_by_side(pairs_T[:]))
+
+        wfc_grouped = const.tile([P, F, PACK], BF16, align_bytes=64)
+        for a in range(F // P):
+            singles_T = psum.tile([P, PACK, P], BF16)
+            transpose_singles(nc, singles_T, wfc_rows[:, a, :], identity_bf16[:])
+            copy_engine(a)(out=wfc_grouped[:, a * P : (a + 1) * P, :], in_=singles_side_by_side(singles_T[:]))
+
+        wo_codes = const.tile([P, PASSES_1 * D], U32, align_bytes=64)
+        wo_scales = const.tile([P, PASSES_1 * D], U8, align_bytes=64)
+        nc.vector.quantize_mx(out=wo_codes[:].bitcast(FP8X4), scales=wo_scales[:], in_=wo_grouped[:])
+        wfc_codes = const.tile([P, F], U32, align_bytes=64)
+        wfc_scales = const.tile([P, F], U8, align_bytes=64)
+        nc.vector.quantize_mx(
+            out=wfc_codes[:].bitcast(FP8X4), scales=wfc_scales[:], in_=wfc_grouped[:].rearrange("p r t -> p (r t)")
+        )
+
+        gain_bank = psum.tile([P, D], F32, tag="attn")
+        nc.tensor.matmul(out=gain_bank[:], lhsT=ones[:], rhs=gain_rows[:], start=True, stop=True)
+        gain = const.tile([P, D], F32)
+        nc.vector.tensor_copy(out=gain[:], in_=gain_bank[:])
+
+        y_rows_of, y_bank_of, y_grouped_of, y_quantised_of, attn_of = {}, {}, {}, {}, {}
+        gained_of, x_mid_of, sum_sq_of, rms_of, inv_rms_of = {}, {}, {}, {}, {}
+        xn_of, xn_bank_of, xn_grouped_of, xn_quantised_of, z_of, relu_of, h_of = {}, {}, {}, {}, {}, {}, {}
+
+        def store_slot(i):
+            return i % TILES_PER_STORE
+
+        def store(dram, i, staged):
+            first = i % TILES_PER_CHUNK - (TILES_PER_STORE - 1)
+            rows = token_rows(dram, i // TILES_PER_CHUNK)[:, first : first + TILES_PER_STORE, :]
+            nc.sync.dma_start(out=rows, in_=staged[:])
+
+        def gather_heads(i):
+            y_rows = work.tile([P, E], BF16)
+            nc.vector.tensor_copy(
+                out=y_rows[:].rearrange("p (h j) -> p h j", h=H),
+                in_=y_chunks[i // TILES_PER_CHUNK][:, :, i % TILES_PER_CHUNK, :],
+            )
+            y_rows_of[i] = y_rows
+
+        def transpose_y(i):
+            pairs_T = psum.tile([P, PACK, P], F32)
+            transpose_pairs(nc, pairs_T, y_rows_of[i][:], identity_f32[:])
+            y_bank_of[i] = pairs_T
+
+        def copy_y_out(i):
+            y_grouped = work.tile([P, E], BF16, align_bytes=64)
+            copy_engine(i)(
+                out=y_grouped[:].bitcast(F32).rearrange("p (g r u) -> p g r u", g=PASSES_1, u=2),
+                in_=pairs_side_by_side(y_bank_of[i][:]),
+            )
+            y_grouped_of[i] = y_grouped
+
+        def quantise_y(i):
+            y_codes = work.tile([P, PASSES_1 * P], U32, align_bytes=64)
+            y_scales = work.tile([P, PASSES_1 * P], U8, align_bytes=64)
+            nc.vector.quantize_mx(out=y_codes[:].bitcast(FP8X4), scales=y_scales[:], in_=y_grouped_of[i][:])
+            y_quantised_of[i] = (y_codes, y_scales)
+
+        def project_heads(i):
+            y_codes, y_scales = y_quantised_of[i]
+            attn = psum.tile([P, D], F32)
+            for g in range(PASSES_1):
+                nc.tensor.matmul_mx(
+                    out=attn[:],
+                    lhsT=y_codes[:, g * P : (g + 1) * P].bitcast(FP8X4),
+                    lhsT_scale=y_scales[:, g * P : (g + 1) * P],
+                    rhs=wo_codes[:, g * D : (g + 1) * D].bitcast(FP8X4),
+                    rhs_scale=wo_scales[:, g * D : (g + 1) * D],
+                    start=(g == 0),
+                    stop=(g == PASSES_1 - 1),
+                )
+            attn_of[i] = attn
+
+        def apply_gain(i):
+            gained = work.tile([P, D], F32)
+            nc.vector.tensor_tensor(out=gained[:], in0=attn_of[i][:], in1=gain[:], op=ALU.mult)
+            gained_of[i] = gained
+
+        def add_residual(i):
+            if store_slot(i) == 0:
+                x_mid_group = results.tile([P, TILES_PER_STORE, D], F32)
+                x_mid_of[i] = x_mid_group
+            else:
+                x_mid_of[i] = x_mid_of[i - 1]
+            nc.vector.tensor_tensor(
+                out=x_mid_of[i][:, store_slot(i), :],
+                in0=gained_of[i][:],
+                in1=x_chunks[i // TILES_PER_CHUNK][:, i % TILES_PER_CHUNK, :],
+                op=ALU.add,
+            )
+            if store_slot(i) == TILES_PER_STORE - 1:
+                store(out_0, i, x_mid_of[i])
+
+        def sum_squares(i):
+            squares = work.tile([P, D], F32)
+            sum_sq = work.tile([P, 1], F32)
+            nc.scalar.activation(
+                out=squares[:], in_=x_mid_of[i][:, store_slot(i), :], func=ACT.Square, accum_out=sum_sq[:]
+            )
+            sum_sq_of[i] = sum_sq
+
+        def root_mean_square(i):
+            rms = work.tile([P, 1], F32)
+            nc.scalar.activation(out=rms[:], in_=sum_sq_of[i][:], func=ACT.Sqrt, bias=eps[:], scale=1.0 / D)
+            rms_of[i] = rms
+
+        def invert_rms(i):
+            inv_rms = work.tile([P, 1], F32)
+            nc.vector.reciprocal(out=inv_rms[:], in_=rms_of[i][:])
+            inv_rms_of[i] = inv_rms
+
+        def normalise(i):
+            xn = work.tile([P, D], BF16)
+            nc.vector.tensor_scalar_mul(
+                out=xn[:], in0=x_mid_of[i][:, store_slot(i), :], scalar1=inv_rms_of[i][:]
+            )
+            xn_of[i] = xn
+
+        def transpose_xn(i):
+            singles_T = psum.tile([P, PACK, P], BF16)
+            transpose_singles(nc, singles_T, xn_of[i][:], identity_bf16[:])
+            xn_bank_of[i] = singles_T
+
+        def copy_xn_out(i):
+            xn_grouped = work.tile([P, P, PACK], BF16, align_bytes=64)
+            nc.scalar.copy(out=xn_grouped[:], in_=singles_side_by_side(xn_bank_of[i][:]))
+            xn_grouped_of[i] = xn_grouped
+
+        def quantise_xn(i):
+            xn_codes = work.tile([P, P], U32, align_bytes=64)
+            xn_scales = work.tile([P, P], U8, align_bytes=64)
+            nc.vector.quantize_mx(
+                out=xn_codes[:].bitcast(FP8X4),
+                scales=xn_scales[:],
+                in_=xn_grouped_of[i][:].rearrange("p r t -> p (r t)"),
+            )
+            xn_quantised_of[i] = (xn_codes, xn_scales)
+
+        def project_up(i):
+            xn_codes, xn_scales = xn_quantised_of[i]
+            z = psum.tile([P, F], F32)
+            nc.tensor.matmul_mx(
+                out=z[:],
+                lhsT=xn_codes[:].bitcast(FP8X4),
+                lhsT_scale=xn_scales[:],
+                rhs=wfc_codes[:].bitcast(FP8X4),
+                rhs_scale=wfc_scales[:],
+                start=True,
+                stop=True,
+            )
+            z_of[i] = z
+
+        def relu(i):
+            positive = work.tile([P, F], F32)
+            nc.scalar.activation(out=positive[:], in_=z_of[i][:], func=ACT.Relu)
+            relu_of[i] = positive
+
+        def square(i):
+            if store_slot(i) == 0:
+                h_group = results.tile([P, TILES_PER_STORE, F], F32)
+                h_of[i] = h_group
+            else:
+                h_of[i] = h_of[i - 1]
+            nc.scalar.activation(out=h_of[i][:, store_slot(i), :], in_=relu_of[i][:], func=ACT.Square)
+            if store_slot(i) == TILES_PER_STORE - 1:
+                store(out_1, i, h_of[i])
+
+        def run(stage, i):
+            if 0 <= i < N_TILES:
+                stage(i)
+
+        (
+            GATHER,
+            TRANSPOSE_Y,
+            COPY_Y,
+            QUANTISE_Y,
+            PROJECT_HEADS,
+            RESIDUAL,
+            STATISTICS,
+            NORMALISE,
+            TRANSPOSE_XN,
+            COPY_XN,
+            QUANTISE_XN,
+            PROJECT_UP,
+            ACTIVATE,
+        ) = range(N_STAGES)
+
+        for step in range(N_TILES + N_STAGES - 1):
+            run(invert_rms, step - NORMALISE)
+            run(transpose_xn, step - TRANSPOSE_XN)
+            run(transpose_y, step - TRANSPOSE_Y)
+            run(project_heads, step - PROJECT_HEADS)
+            run(project_up, step - PROJECT_UP)
+            run(relu, step - ACTIVATE)
+            run(apply_gain, step - RESIDUAL)
+            run(sum_squares, step - STATISTICS)
+            run(gather_heads, step - GATHER)
+            run(add_residual, step - RESIDUAL)
+            run(square, step - ACTIVATE)
+            run(root_mean_square, step - STATISTICS)
+            run(normalise, step - NORMALISE)
+            run(copy_xn_out, step - COPY_XN)
+            run(copy_y_out, step - COPY_Y)
+            run(quantise_xn, step - QUANTISE_XN)
+            run(quantise_y, step - QUANTISE_Y)

@@ -22,131 +22,149 @@ F = 512
 EPS = 1e-6
 
 PASSES_1 = E // K_PASS
-TILES_PER_CHUNK = 8
-CHUNK_TOKENS = P * TILES_PER_CHUNK
-CHUNKS_PER_BATCH = S // CHUNK_TOKENS
-N_CHUNKS = B * CHUNKS_PER_BATCH
-N_TILES = N_CHUNKS * TILES_PER_CHUNK
+TILES_OF_CHUNK = ((2, 2, 4, 8), (8, 8))
+N_TILES = B * S // P
 TILES_PER_STORE = 2
-N_STAGES = 13
+N_STEPS_DEEP = 6
 
 FLOPS = 2 * B * S * E * D + 2 * B * S * D * F
 
 
 def transpose_pairs(nc, bank, rows, identity_f32):
     words = rows.bitcast(F32)
-    for q in range(E // (2 * P)):
+    for q in range(words.shape[1] // P):
         nc.tensor.transpose(bank[:, q, :], words[:, q * P : (q + 1) * P], identity_f32)
-
-
-def transpose_singles(nc, bank, rows, identity_bf16):
-    for t in range(PACK):
-        nc.tensor.transpose(bank[:, t, :], rows[:, t * P : (t + 1) * P], identity_bf16)
 
 
 def pairs_side_by_side(bank):
     return bank.rearrange("p (g u) r -> p g r u", u=2)
 
 
-def singles_side_by_side(bank):
-    return bank.rearrange("p t r -> p r t")
-
-
 def tile_shepherdembryo_pb_t_kernel(tc, y_attn, x, w_o, attn_scale, w_fc, out_0, out_1):
     nc = tc.nc
 
+    chunks = []
+    chunk_of, slot_of = [], []
+    for b, sizes in enumerate(TILES_OF_CHUNK):
+        first_token = 0
+        for tiles in sizes:
+            chunk_of += [len(chunks)] * tiles
+            slot_of += range(tiles)
+            chunks.append((b, first_token, tiles))
+            first_token += tiles * P
+
     def token_rows(dram, chunk):
-        b, part = divmod(chunk, CHUNKS_PER_BATCH)
-        rows = dram[b, part * CHUNK_TOKENS : (part + 1) * CHUNK_TOKENS, :]
-        return rows.rearrange("(p i) d -> p i d", i=TILES_PER_CHUNK)
+        b, first_token, tiles = chunks[chunk]
+        rows = dram[b, first_token : first_token + tiles * P, :]
+        return rows.rearrange("(p i) d -> p i d", i=tiles)
 
     with ExitStack() as stack:
         stack.enter_context(tc.manual_schedule())
         const = stack.enter_context(tc.tile_pool(name="const", bufs=1))
-        resident = stack.enter_context(tc.tile_pool(name="resident", bufs=N_CHUNKS))
         work = stack.enter_context(tc.tile_pool(name="work", bufs=3))
         results = stack.enter_context(tc.tile_pool(name="results", bufs=4))
         psum = stack.enter_context(tc.psum_pool(name="psum", bufs=2))
 
         identity_f32 = const.tile([P, P], F32)
         make_identity(nc, identity_f32[:])
-        identity_bf16 = const.tile([P, P], BF16)
-        make_identity(nc, identity_bf16[:])
         ones = const.tile([P, P], BF16)
         nc.vector.memset(ones[:], 1.0)
         eps = const.tile([P, 1], F32)
         nc.vector.memset(eps[:], EPS)
+        table_loader = const.tile([P, 1], F32)
+        nc.scalar.activation(out=table_loader[:], in_=eps[:], func=ACT.Abs_reciprocal_sqrt)
         gain_rows = const.tile([P, D], BF16)
         nc.vector.memset(gain_rows[:], 0.0)
 
-        wo_rows = const.tile([P, D // P, E], BF16)
-        nc.sync.dma_start(out=wo_rows[:], in_=w_o.rearrange("(a p) k -> p a k", p=P))
-        wfc_rows = const.tile([P, F // P, D], BF16)
-        nc.sync.dma_start(out=wfc_rows[:], in_=w_fc.rearrange("(a p) k -> p a k", p=P))
-        nc.sync.dma_start(out=gain_rows[0:1, :], in_=attn_scale.rearrange("(o d) -> o d", o=1))
-        y_chunks = []
-        x_chunks = []
-        for chunk in range(N_CHUNKS):
-            b, part = divmod(chunk, CHUNKS_PER_BATCH)
-            y_chunk = resident.tile([P, H, TILES_PER_CHUNK, DH], BF16)
+        y_chunks, x_chunks = {}, {}
+
+        def load_y(chunk):
+            b, first_token, tiles = chunks[chunk]
+            y_chunk = const.tile([P, H, tiles, DH], BF16, name="y_chunk_%d" % chunk)
             nc.sync.dma_start(
                 out=y_chunk[:],
-                in_=y_attn[b, :, part * CHUNK_TOKENS : (part + 1) * CHUNK_TOKENS, :].rearrange(
-                    "h (p i) j -> p h i j", i=TILES_PER_CHUNK
+                in_=y_attn[b, :, first_token : first_token + tiles * P, :].rearrange(
+                    "h (p i) j -> p h i j", i=tiles
                 ),
             )
-            y_chunks.append(y_chunk)
-            x_chunk = resident.tile([P, TILES_PER_CHUNK, D], BF16)
+            y_chunks[chunk] = y_chunk
+
+        def load_x(chunk):
+            x_chunk = const.tile([P, chunks[chunk][2], D], BF16, name="x_chunk_%d" % chunk)
             nc.sync.dma_start(out=x_chunk[:], in_=token_rows(x, chunk))
-            x_chunks.append(x_chunk)
+            x_chunks[chunk] = x_chunk
 
-        def copy_engine(piece):
-            return nc.scalar.copy if piece % 2 == 0 else nc.vector.tensor_copy
+        load_y(0)
+        wo_rows = []
+        for g in range(PASSES_1):
+            wo_rows_g = const.tile([P, D // P, K_PASS], BF16, name="wo_rows_%d" % g)
+            nc.sync.dma_start(
+                out=wo_rows_g[:], in_=w_o[:, g * K_PASS : (g + 1) * K_PASS].rearrange("(a p) k -> p a k", p=P)
+            )
+            wo_rows.append(wo_rows_g)
+        nc.sync.dma_start(out=gain_rows[0:1, :], in_=attn_scale.rearrange("(o d) -> o d", o=1))
+        load_y(1)
+        load_x(0)
+        load_x(1)
+        wfc_rows = const.tile([P, F // P, D], BF16)
+        nc.sync.dma_start(out=wfc_rows[:], in_=w_fc.rearrange("(a p) k -> p a k", p=P))
+        for chunk in range(2, len(chunks)):
+            load_y(chunk)
+            load_x(chunk)
 
-        wo_grouped = const.tile([P, PASSES_1 * D * PACK], BF16, align_bytes=64)
-        wo_grouped_words = wo_grouped[:].bitcast(F32).rearrange("p (g r u) -> p g r u", g=PASSES_1, u=2)
-        for a in range(D // P):
-            pairs_T = psum.tile([P, PACK, P], F32)
-            transpose_pairs(nc, pairs_T, wo_rows[:, a, :], identity_f32[:])
-            copy_engine(a)(out=wo_grouped_words[:, :, a * P : (a + 1) * P, :], in_=pairs_side_by_side(pairs_T[:]))
+        def prepare_weights(rows, name):
+            grouped = const.tile([P, D * PACK], BF16, align_bytes=64, name=name + "_grouped")
+            words = grouped[:].bitcast(F32).rearrange("p (a r u) -> p a r u", a=D // P, u=2)
+            for half in range(2):
+                pairs_T = psum.tile([P, PACK, P], F32)
+                for a in range(2):
+                    transpose_pairs(nc, pairs_T[:, 2 * a : 2 * a + 2, :], rows[:, 2 * half + a, :], identity_f32[:])
+                copy = nc.scalar.copy if half == 0 else nc.vector.tensor_copy
+                copy(
+                    out=words[:, 2 * half : 2 * half + 2, :, :],
+                    in_=pairs_T[:].rearrange("p (a u) r -> p a r u", u=2),
+                )
+            codes = const.tile([P, D], U32, align_bytes=64, name=name + "_codes")
+            scales = const.tile([P, D], U8, align_bytes=64, name=name + "_scales")
+            nc.vector.quantize_mx(out=codes[:].bitcast(FP8X4), scales=scales[:], in_=grouped[:])
+            return codes, scales
 
-        wfc_grouped = const.tile([P, F, PACK], BF16, align_bytes=64)
-        for a in range(F // P):
-            singles_T = psum.tile([P, PACK, P], BF16)
-            transpose_singles(nc, singles_T, wfc_rows[:, a, :], identity_bf16[:])
-            copy_engine(a)(out=wfc_grouped[:, a * P : (a + 1) * P, :], in_=singles_side_by_side(singles_T[:]))
+        wo_quantised, wfc_quantised = [], []
 
-        wo_codes = const.tile([P, PASSES_1 * D], U32, align_bytes=64)
-        wo_scales = const.tile([P, PASSES_1 * D], U8, align_bytes=64)
-        nc.vector.quantize_mx(out=wo_codes[:].bitcast(FP8X4), scales=wo_scales[:], in_=wo_grouped[:])
-        wfc_codes = const.tile([P, F], U32, align_bytes=64)
-        wfc_scales = const.tile([P, F], U8, align_bytes=64)
-        nc.vector.quantize_mx(
-            out=wfc_codes[:].bitcast(FP8X4), scales=wfc_scales[:], in_=wfc_grouped[:].rearrange("p r t -> p (r t)")
-        )
+        def prepare_wo():
+            for g in range(PASSES_1):
+                wo_quantised.append(prepare_weights(wo_rows[g], "wo_%d" % g))
 
-        gain_bank = psum.tile([P, D], F32, tag="attn")
-        nc.tensor.matmul(out=gain_bank[:], lhsT=ones[:], rhs=gain_rows[:], start=True, stop=True)
+        def prepare_wfc():
+            wfc_quantised.append(prepare_weights(wfc_rows, "wfc"))
+
         gain = const.tile([P, D], F32)
-        nc.vector.tensor_copy(out=gain[:], in_=gain_bank[:])
+
+        def prepare_gain():
+            attn = psum.tile([P, D], F32)
+            nc.tensor.matmul(out=attn[:], lhsT=ones[:], rhs=gain_rows[:], start=True, stop=True)
+            nc.vector.tensor_copy(out=gain[:], in_=attn[:])
+
+        def y_on_vector(i):
+            return i % 3 == 2
 
         y_rows_of, y_bank_of, y_grouped_of, y_quantised_of, attn_of = {}, {}, {}, {}, {}
-        gained_of, x_mid_of, sum_sq_of, rms_of, inv_rms_of = {}, {}, {}, {}, {}
+        gained_of, x_mid_of, sum_sq_of, inv_rms_of = {}, {}, {}, {}
         xn_of, xn_bank_of, xn_grouped_of, xn_quantised_of, z_of, relu_of, h_of = {}, {}, {}, {}, {}, {}, {}
 
         def store_slot(i):
             return i % TILES_PER_STORE
 
         def store(dram, i, staged):
-            first = i % TILES_PER_CHUNK - (TILES_PER_STORE - 1)
-            rows = token_rows(dram, i // TILES_PER_CHUNK)[:, first : first + TILES_PER_STORE, :]
+            first = slot_of[i] - (TILES_PER_STORE - 1)
+            rows = token_rows(dram, chunk_of[i])[:, first : first + TILES_PER_STORE, :]
             nc.sync.dma_start(out=rows, in_=staged[:])
 
         def gather_heads(i):
             y_rows = work.tile([P, E], BF16)
             nc.vector.tensor_copy(
                 out=y_rows[:].rearrange("p (h j) -> p h j", h=H),
-                in_=y_chunks[i // TILES_PER_CHUNK][:, :, i % TILES_PER_CHUNK, :],
+                in_=y_chunks[chunk_of[i]][:, :, slot_of[i], :],
             )
             y_rows_of[i] = y_rows
 
@@ -157,7 +175,8 @@ def tile_shepherdembryo_pb_t_kernel(tc, y_attn, x, w_o, attn_scale, w_fc, out_0,
 
         def copy_y_out(i):
             y_grouped = work.tile([P, E], BF16, align_bytes=64)
-            copy_engine(i)(
+            copy = nc.vector.tensor_copy if y_on_vector(i) else nc.scalar.copy
+            copy(
                 out=y_grouped[:].bitcast(F32).rearrange("p (g r u) -> p g r u", g=PASSES_1, u=2),
                 in_=pairs_side_by_side(y_bank_of[i][:]),
             )
@@ -172,13 +191,13 @@ def tile_shepherdembryo_pb_t_kernel(tc, y_attn, x, w_o, attn_scale, w_fc, out_0,
         def project_heads(i):
             y_codes, y_scales = y_quantised_of[i]
             attn = psum.tile([P, D], F32)
-            for g in range(PASSES_1):
+            for g, (wo_codes, wo_scales) in enumerate(wo_quantised):
                 nc.tensor.matmul_mx(
                     out=attn[:],
                     lhsT=y_codes[:, g * P : (g + 1) * P].bitcast(FP8X4),
                     lhsT_scale=y_scales[:, g * P : (g + 1) * P],
-                    rhs=wo_codes[:, g * D : (g + 1) * D].bitcast(FP8X4),
-                    rhs_scale=wo_scales[:, g * D : (g + 1) * D],
+                    rhs=wo_codes[:].bitcast(FP8X4),
+                    rhs_scale=wo_scales[:],
                     start=(g == 0),
                     stop=(g == PASSES_1 - 1),
                 )
@@ -198,7 +217,7 @@ def tile_shepherdembryo_pb_t_kernel(tc, y_attn, x, w_o, attn_scale, w_fc, out_0,
             nc.vector.tensor_tensor(
                 out=x_mid_of[i][:, store_slot(i), :],
                 in0=gained_of[i][:],
-                in1=x_chunks[i // TILES_PER_CHUNK][:, i % TILES_PER_CHUNK, :],
+                in1=x_chunks[chunk_of[i]][:, slot_of[i], :],
                 op=ALU.add,
             )
             if store_slot(i) == TILES_PER_STORE - 1:
@@ -212,14 +231,11 @@ def tile_shepherdembryo_pb_t_kernel(tc, y_attn, x, w_o, attn_scale, w_fc, out_0,
             )
             sum_sq_of[i] = sum_sq
 
-        def root_mean_square(i):
-            rms = work.tile([P, 1], F32)
-            nc.scalar.activation(out=rms[:], in_=sum_sq_of[i][:], func=ACT.Sqrt, bias=eps[:], scale=1.0 / D)
-            rms_of[i] = rms
-
         def invert_rms(i):
             inv_rms = work.tile([P, 1], F32)
-            nc.vector.reciprocal(out=inv_rms[:], in_=rms_of[i][:])
+            nc.scalar.activation(
+                out=inv_rms[:], in_=sum_sq_of[i][:], func=ACT.Abs_reciprocal_sqrt, bias=eps[:], scale=1.0 / D
+            )
             inv_rms_of[i] = inv_rms
 
         def normalise(i):
@@ -230,13 +246,16 @@ def tile_shepherdembryo_pb_t_kernel(tc, y_attn, x, w_o, attn_scale, w_fc, out_0,
             xn_of[i] = xn
 
         def transpose_xn(i):
-            singles_T = psum.tile([P, PACK, P], BF16)
-            transpose_singles(nc, singles_T, xn_of[i][:], identity_bf16[:])
-            xn_bank_of[i] = singles_T
+            xn_T = psum.tile([P, 2, P], F32)
+            transpose_pairs(nc, xn_T, xn_of[i][:], identity_f32[:])
+            xn_bank_of[i] = xn_T
 
         def copy_xn_out(i):
-            xn_grouped = work.tile([P, P, PACK], BF16, align_bytes=64)
-            nc.scalar.copy(out=xn_grouped[:], in_=singles_side_by_side(xn_bank_of[i][:]))
+            xn_grouped = work.tile([P, D], BF16, align_bytes=64)
+            nc.scalar.copy(
+                out=xn_grouped[:].bitcast(F32).rearrange("p (r u) -> p r u", u=2),
+                in_=xn_bank_of[i][:].rearrange("p u r -> p r u"),
+            )
             xn_grouped_of[i] = xn_grouped
 
         def quantise_xn(i):
@@ -245,12 +264,13 @@ def tile_shepherdembryo_pb_t_kernel(tc, y_attn, x, w_o, attn_scale, w_fc, out_0,
             nc.vector.quantize_mx(
                 out=xn_codes[:].bitcast(FP8X4),
                 scales=xn_scales[:],
-                in_=xn_grouped_of[i][:].rearrange("p r t -> p (r t)"),
+                in_=xn_grouped_of[i][:],
             )
             xn_quantised_of[i] = (xn_codes, xn_scales)
 
         def project_up(i):
             xn_codes, xn_scales = xn_quantised_of[i]
+            wfc_codes, wfc_scales = wfc_quantised[0]
             z = psum.tile([P, F], F32)
             nc.tensor.matmul_mx(
                 out=z[:],
@@ -282,37 +302,28 @@ def tile_shepherdembryo_pb_t_kernel(tc, y_attn, x, w_o, attn_scale, w_fc, out_0,
             if 0 <= i < N_TILES:
                 stage(i)
 
-        (
-            GATHER,
-            TRANSPOSE_Y,
-            COPY_Y,
-            QUANTISE_Y,
-            PROJECT_HEADS,
-            RESIDUAL,
-            STATISTICS,
-            NORMALISE,
-            TRANSPOSE_XN,
-            COPY_XN,
-            QUANTISE_XN,
-            PROJECT_UP,
-            ACTIVATE,
-        ) = range(N_STAGES)
-
-        for step in range(N_TILES + N_STAGES - 1):
-            run(invert_rms, step - NORMALISE)
-            run(transpose_xn, step - TRANSPOSE_XN)
-            run(transpose_y, step - TRANSPOSE_Y)
-            run(project_heads, step - PROJECT_HEADS)
-            run(project_up, step - PROJECT_UP)
-            run(relu, step - ACTIVATE)
-            run(apply_gain, step - RESIDUAL)
-            run(sum_squares, step - STATISTICS)
-            run(gather_heads, step - GATHER)
-            run(add_residual, step - RESIDUAL)
-            run(square, step - ACTIVATE)
-            run(root_mean_square, step - STATISTICS)
-            run(normalise, step - NORMALISE)
-            run(copy_xn_out, step - COPY_XN)
-            run(copy_y_out, step - COPY_Y)
-            run(quantise_xn, step - QUANTISE_XN)
-            run(quantise_y, step - QUANTISE_Y)
+        for step in range(N_TILES + N_STEPS_DEEP):
+            run(sum_squares, step - 3)
+            run(transpose_xn, step - 4)
+            run(gather_heads, step)
+            run(transpose_y, step)
+            run(project_up, step - 5)
+            run(apply_gain, step - 2)
+            run(quantise_y, step - 1)
+            run(project_heads, step - 1)
+            run(square, step - 6)
+            run(invert_rms, step - 3)
+            run(copy_xn_out, step - 4)
+            run(add_residual, step - 2)
+            if not y_on_vector(step):
+                run(copy_y_out, step)
+            run(normalise, step - 3)
+            run(quantise_xn, step - 4)
+            if y_on_vector(step):
+                run(copy_y_out, step)
+            run(relu, step - 5)
+            if step == 0:
+                prepare_wo()
+                prepare_gain()
+            if step == 3:
+                prepare_wfc()

@@ -22,10 +22,11 @@ F = 512
 EPS = 1e-6
 
 PASSES_1 = E // K_PASS
-TILES_OF_CHUNK = ((2, 2, 4, 8), (8, 8))
+GROUP = 2
 N_TILES = B * S // P
-TILES_PER_STORE = 2
-N_STEPS_DEEP = 6
+N_GROUPS = N_TILES // GROUP
+TILES_OF_CHUNK = ((2, 2, 4, 8), (8, 8))
+FIRST_SHARED_GROUP = N_GROUPS - 4
 
 FLOPS = 2 * B * S * E * D + 2 * B * S * D * F
 
@@ -34,10 +35,6 @@ def transpose_pairs(nc, bank, rows, identity_f32):
     words = rows.bitcast(F32)
     for q in range(words.shape[1] // P):
         nc.tensor.transpose(bank[:, q, :], words[:, q * P : (q + 1) * P], identity_f32)
-
-
-def pairs_side_by_side(bank):
-    return bank.rearrange("p (g u) r -> p g r u", u=2)
 
 
 def tile_shepherdembryo_pb_t_kernel(tc, y_attn, x, w_o, attn_scale, w_fc, out_0, out_1):
@@ -61,20 +58,9 @@ def tile_shepherdembryo_pb_t_kernel(tc, y_attn, x, w_o, attn_scale, w_fc, out_0,
     with ExitStack() as stack:
         stack.enter_context(tc.manual_schedule())
         const = stack.enter_context(tc.tile_pool(name="const", bufs=1))
-        work = stack.enter_context(tc.tile_pool(name="work", bufs=3))
+        work = stack.enter_context(tc.tile_pool(name="work", bufs=2))
         results = stack.enter_context(tc.tile_pool(name="results", bufs=4))
         psum = stack.enter_context(tc.psum_pool(name="psum", bufs=2))
-
-        identity_f32 = const.tile([P, P], F32)
-        make_identity(nc, identity_f32[:])
-        ones = const.tile([P, P], BF16)
-        nc.vector.memset(ones[:], 1.0)
-        eps = const.tile([P, 1], F32)
-        nc.vector.memset(eps[:], EPS)
-        table_loader = const.tile([P, 1], F32)
-        nc.scalar.activation(out=table_loader[:], in_=eps[:], func=ACT.Abs_reciprocal_sqrt)
-        gain_rows = const.tile([P, D], BF16)
-        nc.vector.memset(gain_rows[:], 0.0)
 
         y_chunks, x_chunks = {}, {}
 
@@ -102,228 +88,279 @@ def tile_shepherdembryo_pb_t_kernel(tc, y_attn, x, w_o, attn_scale, w_fc, out_0,
                 out=wo_rows_g[:], in_=w_o[:, g * K_PASS : (g + 1) * K_PASS].rearrange("(a p) k -> p a k", p=P)
             )
             wo_rows.append(wo_rows_g)
+        gain_rows = const.tile([P, D], BF16)
+        nc.vector.memset(gain_rows[:], 0.0)
         nc.sync.dma_start(out=gain_rows[0:1, :], in_=attn_scale.rearrange("(o d) -> o d", o=1))
         load_y(1)
         load_x(0)
-        load_x(1)
+        load_y(2)
         wfc_rows = const.tile([P, F // P, D], BF16)
         nc.sync.dma_start(out=wfc_rows[:], in_=w_fc.rearrange("(a p) k -> p a k", p=P))
-        for chunk in range(2, len(chunks)):
+        load_x(1)
+        load_x(2)
+        for chunk in range(3, len(chunks)):
             load_y(chunk)
             load_x(chunk)
 
-        def prepare_weights(rows, name):
-            grouped = const.tile([P, D * PACK], BF16, align_bytes=64, name=name + "_grouped")
-            words = grouped[:].bitcast(F32).rearrange("p (a r u) -> p a r u", a=D // P, u=2)
-            for half in range(2):
-                pairs_T = psum.tile([P, PACK, P], F32)
-                for a in range(2):
-                    transpose_pairs(nc, pairs_T[:, 2 * a : 2 * a + 2, :], rows[:, 2 * half + a, :], identity_f32[:])
-                copy = nc.scalar.copy if half == 0 else nc.vector.tensor_copy
-                copy(
-                    out=words[:, 2 * half : 2 * half + 2, :, :],
-                    in_=pairs_T[:].rearrange("p (a u) r -> p a r u", u=2),
-                )
+        identity_f32 = const.tile([P, P], F32)
+        make_identity(nc, identity_f32[:])
+        ones = const.tile([P, P], BF16)
+        nc.vector.memset(ones[:], 1.0)
+        eps = const.tile([P, 1], F32)
+        nc.vector.memset(eps[:], EPS)
+        table_loader = const.tile([P, 1], F32)
+        nc.scalar.activation(out=table_loader[:], in_=eps[:], func=ACT.Abs_reciprocal_sqrt)
+
+        weight_banks = {}
+
+        def transpose_weights(name, rows, half, tag):
+            bank = psum.tile([P, PACK, P], F32, tag=tag, name="%s_%d_T" % (name, half))
+            for a in range(2):
+                transpose_pairs(nc, bank[:, 2 * a : 2 * a + 2, :], rows[:, 2 * half + a, :], identity_f32[:])
+            weight_banks[name, half] = bank
+
+        grouped_weights = {}
+
+        def copy_weights_out(name, half, copy):
+            if half == 0:
+                grouped = const.tile([P, D * PACK], BF16, align_bytes=64, name=name + "_grouped")
+                grouped_weights[name] = grouped
+            words = grouped_weights[name][:].bitcast(F32).rearrange("p (a r u) -> p a r u", a=D // P, u=2)
+            copy(
+                out=words[:, 2 * half : 2 * half + 2, :, :],
+                in_=weight_banks[name, half][:].rearrange("p (a u) r -> p a r u", u=2),
+            )
+
+        quantised_weights = {}
+
+        def quantise_weights(name):
             codes = const.tile([P, D], U32, align_bytes=64, name=name + "_codes")
             scales = const.tile([P, D], U8, align_bytes=64, name=name + "_scales")
-            nc.vector.quantize_mx(out=codes[:].bitcast(FP8X4), scales=scales[:], in_=grouped[:])
-            return codes, scales
+            nc.vector.quantize_mx(out=codes[:].bitcast(FP8X4), scales=scales[:], in_=grouped_weights[name][:])
+            quantised_weights[name] = (codes, scales)
 
-        wo_quantised, wfc_quantised = [], []
-
-        def prepare_wo():
-            for g in range(PASSES_1):
-                wo_quantised.append(prepare_weights(wo_rows[g], "wo_%d" % g))
-
-        def prepare_wfc():
-            wfc_quantised.append(prepare_weights(wfc_rows, "wfc"))
-
-        gain = const.tile([P, D], F32)
-
-        def prepare_gain():
-            attn = psum.tile([P, D], F32)
-            nc.tensor.matmul(out=attn[:], lhsT=ones[:], rhs=gain_rows[:], start=True, stop=True)
-            nc.vector.tensor_copy(out=gain[:], in_=attn[:])
-
-        def y_on_vector(i):
-            return i % 3 == 2
-
-        y_rows_of, y_bank_of, y_grouped_of, y_quantised_of, attn_of = {}, {}, {}, {}, {}
+        y_rows_of, y_banks_of, y_grouped_of, y_quantised_of, attn_of = {}, {}, {}, {}, {}
         gained_of, x_mid_of, sum_sq_of, inv_rms_of = {}, {}, {}, {}
         xn_of, xn_bank_of, xn_grouped_of, xn_quantised_of, z_of, relu_of, h_of = {}, {}, {}, {}, {}, {}, {}
 
-        def store_slot(i):
-            return i % TILES_PER_STORE
+        def place(j):
+            first = slot_of[GROUP * j]
+            return chunk_of[GROUP * j], slice(first, first + GROUP)
 
-        def store(dram, i, staged):
-            first = slot_of[i] - (TILES_PER_STORE - 1)
-            rows = token_rows(dram, chunk_of[i])[:, first : first + TILES_PER_STORE, :]
-            nc.sync.dma_start(out=rows, in_=staged[:])
-
-        def gather_heads(i):
-            y_rows = work.tile([P, E], BF16)
+        def gather_heads(j):
+            chunk, slots = place(j)
+            y_rows = work.tile([P, GROUP, E], BF16)
             nc.vector.tensor_copy(
-                out=y_rows[:].rearrange("p (h j) -> p h j", h=H),
-                in_=y_chunks[chunk_of[i]][:, :, slot_of[i], :],
+                out=y_rows[:].rearrange("p i (h j) -> p i h j", h=H),
+                in_=y_chunks[chunk][:, :, slots, :].rearrange("p h i j -> p i h j"),
             )
-            y_rows_of[i] = y_rows
+            y_rows_of[j] = y_rows
 
-        def transpose_y(i):
-            pairs_T = psum.tile([P, PACK, P], F32)
-            transpose_pairs(nc, pairs_T, y_rows_of[i][:], identity_f32[:])
-            y_bank_of[i] = pairs_T
+        def transpose_y(j):
+            banks = []
+            for e in range(GROUP):
+                y_T = psum.tile([P, 2 * PASSES_1, P], F32)
+                transpose_pairs(nc, y_T, y_rows_of[j][:, e, :], identity_f32[:])
+                banks.append(y_T)
+            y_banks_of[j] = banks
+            y_grouped = work.tile([P, GROUP, E], BF16, align_bytes=64)
+            y_grouped_of[j] = y_grouped
 
-        def copy_y_out(i):
-            y_grouped = work.tile([P, E], BF16, align_bytes=64)
-            copy = nc.vector.tensor_copy if y_on_vector(i) else nc.scalar.copy
-            copy(
-                out=y_grouped[:].bitcast(F32).rearrange("p (g r u) -> p g r u", g=PASSES_1, u=2),
-                in_=pairs_side_by_side(y_bank_of[i][:]),
-            )
-            y_grouped_of[i] = y_grouped
+        def copy_y_out(j, on_vector):
+            copy = nc.vector.tensor_copy if on_vector else nc.scalar.copy
+            for e in range(GROUP):
+                if ((GROUP * j + e) % 3 == 2) == on_vector:
+                    copy(
+                        out=y_grouped_of[j][:, e, :].bitcast(F32).rearrange("p (g r u) -> p g r u", g=PASSES_1, u=2),
+                        in_=y_banks_of[j][e][:].rearrange("p (g u) r -> p g r u", u=2),
+                    )
 
-        def quantise_y(i):
-            y_codes = work.tile([P, PASSES_1 * P], U32, align_bytes=64)
-            y_scales = work.tile([P, PASSES_1 * P], U8, align_bytes=64)
-            nc.vector.quantize_mx(out=y_codes[:].bitcast(FP8X4), scales=y_scales[:], in_=y_grouped_of[i][:])
-            y_quantised_of[i] = (y_codes, y_scales)
-
-        def project_heads(i):
-            y_codes, y_scales = y_quantised_of[i]
-            attn = psum.tile([P, D], F32)
-            for g, (wo_codes, wo_scales) in enumerate(wo_quantised):
-                nc.tensor.matmul_mx(
-                    out=attn[:],
-                    lhsT=y_codes[:, g * P : (g + 1) * P].bitcast(FP8X4),
-                    lhsT_scale=y_scales[:, g * P : (g + 1) * P],
-                    rhs=wo_codes[:].bitcast(FP8X4),
-                    rhs_scale=wo_scales[:],
-                    start=(g == 0),
-                    stop=(g == PASSES_1 - 1),
-                )
-            attn_of[i] = attn
-
-        def apply_gain(i):
-            gained = work.tile([P, D], F32)
-            nc.vector.tensor_tensor(out=gained[:], in0=attn_of[i][:], in1=gain[:], op=ALU.mult)
-            gained_of[i] = gained
-
-        def add_residual(i):
-            if store_slot(i) == 0:
-                x_mid_group = results.tile([P, TILES_PER_STORE, D], F32)
-                x_mid_of[i] = x_mid_group
-            else:
-                x_mid_of[i] = x_mid_of[i - 1]
-            nc.vector.tensor_tensor(
-                out=x_mid_of[i][:, store_slot(i), :],
-                in0=gained_of[i][:],
-                in1=x_chunks[chunk_of[i]][:, slot_of[i], :],
-                op=ALU.add,
-            )
-            if store_slot(i) == TILES_PER_STORE - 1:
-                store(out_0, i, x_mid_of[i])
-
-        def sum_squares(i):
-            squares = work.tile([P, D], F32)
-            sum_sq = work.tile([P, 1], F32)
-            nc.scalar.activation(
-                out=squares[:], in_=x_mid_of[i][:, store_slot(i), :], func=ACT.Square, accum_out=sum_sq[:]
-            )
-            sum_sq_of[i] = sum_sq
-
-        def invert_rms(i):
-            inv_rms = work.tile([P, 1], F32)
-            nc.scalar.activation(
-                out=inv_rms[:], in_=sum_sq_of[i][:], func=ACT.Abs_reciprocal_sqrt, bias=eps[:], scale=1.0 / D
-            )
-            inv_rms_of[i] = inv_rms
-
-        def normalise(i):
-            xn = work.tile([P, D], BF16)
-            nc.vector.tensor_scalar_mul(
-                out=xn[:], in0=x_mid_of[i][:, store_slot(i), :], scalar1=inv_rms_of[i][:]
-            )
-            xn_of[i] = xn
-
-        def transpose_xn(i):
-            xn_T = psum.tile([P, 2, P], F32)
-            transpose_pairs(nc, xn_T, xn_of[i][:], identity_f32[:])
-            xn_bank_of[i] = xn_T
-
-        def copy_xn_out(i):
-            xn_grouped = work.tile([P, D], BF16, align_bytes=64)
-            nc.scalar.copy(
-                out=xn_grouped[:].bitcast(F32).rearrange("p (r u) -> p r u", u=2),
-                in_=xn_bank_of[i][:].rearrange("p u r -> p r u"),
-            )
-            xn_grouped_of[i] = xn_grouped
-
-        def quantise_xn(i):
-            xn_codes = work.tile([P, P], U32, align_bytes=64)
-            xn_scales = work.tile([P, P], U8, align_bytes=64)
+        def quantise_y(j):
+            y_codes = work.tile([P, GROUP * PASSES_1 * P], U32, align_bytes=64)
+            y_scales = work.tile([P, GROUP * PASSES_1 * P], U8, align_bytes=64)
             nc.vector.quantize_mx(
-                out=xn_codes[:].bitcast(FP8X4),
-                scales=xn_scales[:],
-                in_=xn_grouped_of[i][:],
+                out=y_codes[:].bitcast(FP8X4),
+                scales=y_scales[:],
+                in_=y_grouped_of[j][:].rearrange("p i k -> p (i k)"),
             )
-            xn_quantised_of[i] = (xn_codes, xn_scales)
+            y_quantised_of[j] = (y_codes, y_scales)
 
-        def project_up(i):
-            xn_codes, xn_scales = xn_quantised_of[i]
-            wfc_codes, wfc_scales = wfc_quantised[0]
-            z = psum.tile([P, F], F32)
-            nc.tensor.matmul_mx(
-                out=z[:],
-                lhsT=xn_codes[:].bitcast(FP8X4),
-                lhsT_scale=xn_scales[:],
-                rhs=wfc_codes[:].bitcast(FP8X4),
-                rhs_scale=wfc_scales[:],
-                start=True,
-                stop=True,
+        def project_heads(j):
+            y_codes, y_scales = y_quantised_of[j]
+            banks = []
+            for e in range(GROUP):
+                attn = psum.tile([P, D], F32)
+                for g in range(PASSES_1):
+                    wo_codes, wo_scales = quantised_weights["wo_%d" % g]
+                    columns = slice((e * PASSES_1 + g) * P, (e * PASSES_1 + g + 1) * P)
+                    nc.tensor.matmul_mx(
+                        out=attn[:],
+                        lhsT=y_codes[:, columns].bitcast(FP8X4),
+                        lhsT_scale=y_scales[:, columns],
+                        rhs=wo_codes[:].bitcast(FP8X4),
+                        rhs_scale=wo_scales[:],
+                        start=(g == 0),
+                        stop=(g == PASSES_1 - 1),
+                    )
+                banks.append(attn)
+            attn_of[j] = banks
+
+        def apply_gain(j):
+            gained = work.tile([P, GROUP, D], F32)
+            for e in range(GROUP):
+                nc.vector.tensor_tensor(out=gained[:, e, :], in0=attn_of[j][e][:], in1=gain[:], op=ALU.mult)
+            gained_of[j] = gained
+
+        def add_residual(j):
+            chunk, slots = place(j)
+            x_mid = results.tile([P, GROUP, D], F32)
+            nc.vector.tensor_tensor(
+                out=x_mid[:], in0=gained_of[j][:], in1=x_chunks[chunk][:, slots, :], op=ALU.add
             )
-            z_of[i] = z
+            nc.sync.dma_start(out=token_rows(out_0, chunk)[:, slots, :], in_=x_mid[:])
+            x_mid_of[j] = x_mid
 
-        def relu(i):
-            positive = work.tile([P, F], F32)
-            nc.scalar.activation(out=positive[:], in_=z_of[i][:], func=ACT.Relu)
-            relu_of[i] = positive
+        def sum_squares(j):
+            sum_sq = work.tile([P, GROUP], F32)
+            for e in range(GROUP):
+                squares = work.tile([P, D], F32)
+                nc.scalar.activation(
+                    out=squares[:], in_=x_mid_of[j][:, e, :], func=ACT.Square, accum_out=sum_sq[:, e : e + 1]
+                )
+            sum_sq_of[j] = sum_sq
 
-        def square(i):
-            if store_slot(i) == 0:
-                h_group = results.tile([P, TILES_PER_STORE, F], F32)
-                h_of[i] = h_group
+        def invert_rms(j):
+            inv_rms = work.tile([P, GROUP], F32)
+            nc.scalar.activation(
+                out=inv_rms[:], in_=sum_sq_of[j][:], func=ACT.Abs_reciprocal_sqrt, bias=eps[:], scale=1.0 / D
+            )
+            inv_rms_of[j] = inv_rms
+
+        def normalise(j):
+            xn = work.tile([P, GROUP, D], BF16)
+            for e in range(GROUP):
+                nc.vector.tensor_scalar_mul(
+                    out=xn[:, e, :], in0=x_mid_of[j][:, e, :], scalar1=inv_rms_of[j][:, e : e + 1]
+                )
+            xn_of[j] = xn
+
+        def transpose_xn(j):
+            xn_T = psum.tile([P, PACK, P], F32)
+            for e in range(GROUP):
+                transpose_pairs(nc, xn_T[:, 2 * e : 2 * e + 2, :], xn_of[j][:, e, :], identity_f32[:])
+            xn_bank_of[j] = xn_T
+
+        def copy_xn_out(j):
+            xn_grouped = work.tile([P, GROUP * D], BF16, align_bytes=64)
+            nc.scalar.copy(
+                out=xn_grouped[:].bitcast(F32).rearrange("p (i r u) -> p i r u", i=GROUP, u=2),
+                in_=xn_bank_of[j][:].rearrange("p (i u) r -> p i r u", u=2),
+            )
+            xn_grouped_of[j] = xn_grouped
+
+        def quantise_xn(j):
+            xn_codes = work.tile([P, GROUP * P], U32, align_bytes=64)
+            xn_scales = work.tile([P, GROUP * P], U8, align_bytes=64)
+            nc.vector.quantize_mx(out=xn_codes[:].bitcast(FP8X4), scales=xn_scales[:], in_=xn_grouped_of[j][:])
+            xn_quantised_of[j] = (xn_codes, xn_scales)
+
+        def project_up(j):
+            xn_codes, xn_scales = xn_quantised_of[j]
+            wfc_codes, wfc_scales = quantised_weights["wfc"]
+            banks = []
+            for e in range(GROUP):
+                z = psum.tile([P, F], F32)
+                nc.tensor.matmul_mx(
+                    out=z[:],
+                    lhsT=xn_codes[:, e * P : (e + 1) * P].bitcast(FP8X4),
+                    lhsT_scale=xn_scales[:, e * P : (e + 1) * P],
+                    rhs=wfc_codes[:].bitcast(FP8X4),
+                    rhs_scale=wfc_scales[:],
+                    start=True,
+                    stop=True,
+                )
+                banks.append(z)
+            z_of[j] = banks
+            positive = work.tile([P, GROUP, F], F32)
+            relu_of[j] = positive
+
+        def tiles_of(j, on_vector):
+            return [e for e in range(GROUP) if (j >= FIRST_SHARED_GROUP and e == GROUP - 1) == on_vector]
+
+        def relu(j, on_vector):
+            for e in tiles_of(j, on_vector):
+                if on_vector:
+                    nc.vector.tensor_scalar_max(out=relu_of[j][:, e, :], in0=z_of[j][e][:], scalar1=0.0)
+                else:
+                    nc.scalar.activation(out=relu_of[j][:, e, :], in_=z_of[j][e][:], func=ACT.Relu)
+
+        def square(j, on_vector):
+            tiles = tiles_of(j, on_vector)
+            if not tiles:
+                return
+            if tiles[0] == 0:
+                h = results.tile([P, GROUP, F], F32)
+                h_of[j] = h
+            part = slice(tiles[0], tiles[-1] + 1)
+            positive = relu_of[j][:, part, :]
+            squared = h_of[j][:, part, :]
+            if on_vector:
+                nc.vector.tensor_tensor(out=squared, in0=positive, in1=positive, op=ALU.mult)
             else:
-                h_of[i] = h_of[i - 1]
-            nc.scalar.activation(out=h_of[i][:, store_slot(i), :], in_=relu_of[i][:], func=ACT.Square)
-            if store_slot(i) == TILES_PER_STORE - 1:
-                store(out_1, i, h_of[i])
+                nc.scalar.activation(out=squared, in_=positive, func=ACT.Square)
+            chunk, slots = place(j)
+            rows = token_rows(out_1, chunk)[:, slots, :]
+            nc.sync.dma_start(out=rows[:, part, :], in_=squared)
 
-        def run(stage, i):
-            if 0 <= i < N_TILES:
-                stage(i)
+        def run(stage, j, *arguments):
+            if 0 <= j < N_GROUPS:
+                stage(j, *arguments)
 
-        for step in range(N_TILES + N_STEPS_DEEP):
-            run(sum_squares, step - 3)
-            run(transpose_xn, step - 4)
-            run(gather_heads, step)
-            run(transpose_y, step)
-            run(project_up, step - 5)
-            run(apply_gain, step - 2)
-            run(quantise_y, step - 1)
-            run(project_heads, step - 1)
-            run(square, step - 6)
-            run(invert_rms, step - 3)
-            run(copy_xn_out, step - 4)
-            run(add_residual, step - 2)
-            if not y_on_vector(step):
-                run(copy_y_out, step)
-            run(normalise, step - 3)
-            run(quantise_xn, step - 4)
-            if y_on_vector(step):
-                run(copy_y_out, step)
-            run(relu, step - 5)
-            if step == 0:
-                prepare_wo()
-                prepare_gain()
-            if step == 3:
-                prepare_wfc()
+        gather_heads(0)
+        transpose_y(0)
+        for half in range(2):
+            transpose_weights("wo_0", wo_rows[0], half, "z")
+        for half in range(2):
+            transpose_weights("wo_1", wo_rows[1], half, "xn_T")
+        copy_y_out(0, False)
+        for half in range(2):
+            copy_weights_out("wo_0", half, nc.vector.tensor_copy)
+            copy_weights_out("wo_1", half, nc.scalar.copy)
+        quantise_y(0)
+        quantise_weights("wo_0")
+        quantise_weights("wo_1")
+        gain = const.tile([P, D], F32)
+        gain_bank = psum.tile([P, D], F32, tag="attn")
+        nc.tensor.matmul(out=gain_bank[:], lhsT=ones[:], rhs=gain_rows[:], start=True, stop=True)
+        nc.vector.tensor_copy(out=gain[:], in_=gain_bank[:])
+        project_heads(0)
+        gather_heads(1)
+        transpose_y(1)
+        copy_y_out(1, False)
+        copy_y_out(1, True)
+
+        for step in range(N_GROUPS + 4):
+            run(transpose_xn, step - 2)
+            run(sum_squares, step - 1)
+            run(gather_heads, step + 2)
+            run(transpose_y, step + 2)
+            run(apply_gain, step)
+            run(project_up, step - 3)
+            run(quantise_y, step + 1)
+            run(square, step - 4, False)
+            run(square, step - 4, True)
+            run(invert_rms, step - 1)
+            run(copy_xn_out, step - 2)
+            run(project_heads, step + 1)
+            run(add_residual, step)
+            run(copy_y_out, step + 2, False)
+            run(normalise, step - 1)
+            run(quantise_xn, step - 2)
+            run(copy_y_out, step + 2, True)
+            run(relu, step - 3, False)
+            run(relu, step - 3, True)
+            if step < 2:
+                transpose_weights("wfc", wfc_rows, step, "xn_T")
+                copy_weights_out("wfc", step, nc.scalar.copy)
+            if step == 2:
+                quantise_weights("wfc")

@@ -25,7 +25,8 @@ PASSES_1 = E // K_PASS
 GROUP = 2
 N_TILES = B * S // P
 N_GROUPS = N_TILES // GROUP
-TILES_OF_CHUNK = ((2, 2, 4, 8), (8, 8))
+TILES_OF_CHUNK = ((2, 2, 4, 4, 4), (8, 8))
+LOAD_STEP = {4: 1, 5: 2, 6: 6}
 FIRST_SHARED_GROUP = N_GROUPS - 4
 
 FLOPS = 2 * B * S * E * D + 2 * B * S * D * F
@@ -98,9 +99,8 @@ def tile_shepherdembryo_pb_t_kernel(tc, y_attn, x, w_o, attn_scale, w_fc, out_0,
         nc.sync.dma_start(out=wfc_rows[:], in_=w_fc.rearrange("(a p) k -> p a k", p=P))
         load_x(1)
         load_x(2)
-        for chunk in range(3, len(chunks)):
-            load_y(chunk)
-            load_x(chunk)
+        load_y(3)
+        load_x(3)
 
         identity_f32 = const.tile([P, P], F32)
         make_identity(nc, identity_f32[:])
@@ -169,7 +169,7 @@ def tile_shepherdembryo_pb_t_kernel(tc, y_attn, x, w_o, attn_scale, w_fc, out_0,
         def copy_y_out(j, on_vector):
             copy = nc.vector.tensor_copy if on_vector else nc.scalar.copy
             for e in range(GROUP):
-                if ((GROUP * j + e) % 3 == 2) == on_vector:
+                if ((GROUP * j + e) % 5 == 4) == on_vector:
                     copy(
                         out=y_grouped_of[j][:, e, :].bitcast(F32).rearrange("p (g r u) -> p g r u", g=PASSES_1, u=2),
                         in_=y_banks_of[j][e][:].rearrange("p (g u) r -> p g r u", u=2),
@@ -340,6 +340,10 @@ def tile_shepherdembryo_pb_t_kernel(tc, y_attn, x, w_o, attn_scale, w_fc, out_0,
         copy_y_out(1, True)
 
         for step in range(N_GROUPS + 4):
+            for chunk in LOAD_STEP:
+                if LOAD_STEP[chunk] == step:
+                    load_y(chunk)
+                    load_x(chunk)
             run(transpose_xn, step - 2)
             run(sum_squares, step - 1)
             run(gather_heads, step + 2)

@@ -27,6 +27,7 @@ N_TILES = B * S // P
 N_GROUPS = N_TILES // GROUP
 TILES_OF_CHUNK = ((2, 2, 4, 4, 4), (8, 8))
 LOAD_STEP = {4: 1, 5: 2, 6: 6}
+MERGED_CHUNKS = (5, 6)
 FIRST_SHARED_GROUP = N_GROUPS - 4
 
 FLOPS = 2 * B * S * E * D + 2 * B * S * D * F
@@ -67,13 +68,16 @@ def tile_shepherdembryo_pb_t_kernel(tc, y_attn, x, w_o, attn_scale, w_fc, out_0,
 
         def load_y(chunk):
             b, first_token, tiles = chunks[chunk]
-            y_chunk = const.tile([P, H, tiles, DH], BF16, name="y_chunk_%d" % chunk)
-            nc.sync.dma_start(
-                out=y_chunk[:],
-                in_=y_attn[b, :, first_token : first_token + tiles * P, :].rearrange(
-                    "h (p i) j -> p h i j", i=tiles
-                ),
-            )
+            tokens = y_attn[b, :, first_token : first_token + tiles * P, :]
+            if chunk in MERGED_CHUNKS:
+                y_chunk = const.tile([P, tiles, H, DH], BF16, name="y_chunk_%d" % chunk)
+                for head in range(H):
+                    nc.sync.dma_start(
+                        out=y_chunk[:, :, head, :], in_=tokens[head].rearrange("(p i) j -> p i j", i=tiles)
+                    )
+            else:
+                y_chunk = const.tile([P, H, tiles, DH], BF16, name="y_chunk_%d" % chunk)
+                nc.sync.dma_start(out=y_chunk[:], in_=tokens.rearrange("h (p i) j -> p h i j", i=tiles))
             y_chunks[chunk] = y_chunk
 
         def load_x(chunk):
@@ -149,12 +153,15 @@ def tile_shepherdembryo_pb_t_kernel(tc, y_attn, x, w_o, attn_scale, w_fc, out_0,
 
         def gather_heads(j):
             chunk, slots = place(j)
+            if chunk in MERGED_CHUNKS:
+                y_rows_of[j] = y_chunks[chunk][:, slots, :, :].rearrange("p i h j -> p i (h j)")
+                return
             y_rows = work.tile([P, GROUP, E], BF16)
             nc.vector.tensor_copy(
                 out=y_rows[:].rearrange("p i (h j) -> p i h j", h=H),
                 in_=y_chunks[chunk][:, :, slots, :].rearrange("p h i j -> p i h j"),
             )
-            y_rows_of[j] = y_rows
+            y_rows_of[j] = y_rows[:]
 
         def transpose_y(j):
             banks = []

@@ -27,8 +27,10 @@ N_TILES = B * S // P
 N_GROUPS = N_TILES // GROUP
 TILES_OF_CHUNK = ((2, 2, 4, 4, 4), (8, 8))
 LOAD_STEP = {4: 1, 5: 2, 6: 6}
-MERGED_CHUNKS = (5, 6)
-FIRST_SHARED_GROUP = N_GROUPS - 4
+MERGED_CHUNKS = (3, 4, 5, 6)
+FIRST_SHARED_SQUARE = N_GROUPS - 6
+FIRST_SHARED_RELU = N_GROUPS - 4
+WARM_UP_MATMULS = 20
 
 FLOPS = 2 * B * S * E * D + 2 * B * S * D * F
 
@@ -93,6 +95,8 @@ def tile_shepherdembryo_pb_t_kernel(tc, y_attn, x, w_o, attn_scale, w_fc, out_0,
                 out=wo_rows_g[:], in_=w_o[:, g * K_PASS : (g + 1) * K_PASS].rearrange("(a p) k -> p a k", p=P)
             )
             wo_rows.append(wo_rows_g)
+        ones = const.tile([P, P], BF16)
+        nc.vector.memset(ones[:], 1.0)
         gain_rows = const.tile([P, D], BF16)
         nc.vector.memset(gain_rows[:], 0.0)
         nc.sync.dma_start(out=gain_rows[0:1, :], in_=attn_scale.rearrange("(o d) -> o d", o=1))
@@ -108,10 +112,11 @@ def tile_shepherdembryo_pb_t_kernel(tc, y_attn, x, w_o, attn_scale, w_fc, out_0,
 
         identity_f32 = const.tile([P, P], F32)
         make_identity(nc, identity_f32[:])
-        ones = const.tile([P, P], BF16)
-        nc.vector.memset(ones[:], 1.0)
         eps = const.tile([P, 1], F32)
         nc.vector.memset(eps[:], EPS)
+        warm_up_bank = psum.tile([P, P], F32, tag="attn")
+        for repeat in range(WARM_UP_MATMULS):
+            nc.tensor.matmul(out=warm_up_bank[:], lhsT=ones[:], rhs=ones[:], start=True, stop=True)
         table_loader = const.tile([P, 1], F32)
         nc.scalar.activation(out=table_loader[:], in_=eps[:], func=ACT.Abs_reciprocal_sqrt)
 
@@ -176,7 +181,7 @@ def tile_shepherdembryo_pb_t_kernel(tc, y_attn, x, w_o, attn_scale, w_fc, out_0,
         def copy_y_out(j, on_vector):
             copy = nc.vector.tensor_copy if on_vector else nc.scalar.copy
             for e in range(GROUP):
-                if ((GROUP * j + e) % 5 == 4) == on_vector:
+                if ((GROUP * j + e) % 3 == 2) == on_vector:
                     copy(
                         out=y_grouped_of[j][:, e, :].bitcast(F32).rearrange("p (g r u) -> p g r u", g=PASSES_1, u=2),
                         in_=y_banks_of[j][e][:].rearrange("p (g u) r -> p g r u", u=2),
@@ -291,18 +296,18 @@ def tile_shepherdembryo_pb_t_kernel(tc, y_attn, x, w_o, attn_scale, w_fc, out_0,
             positive = work.tile([P, GROUP, F], F32)
             relu_of[j] = positive
 
-        def tiles_of(j, on_vector):
-            return [e for e in range(GROUP) if (j >= FIRST_SHARED_GROUP and e == GROUP - 1) == on_vector]
+        def tiles_of(j, on_vector, first_shared_group):
+            return [e for e in range(GROUP) if (j >= first_shared_group and e == GROUP - 1) == on_vector]
 
         def relu(j, on_vector):
-            for e in tiles_of(j, on_vector):
+            for e in tiles_of(j, on_vector, FIRST_SHARED_RELU):
                 if on_vector:
                     nc.vector.tensor_scalar_max(out=relu_of[j][:, e, :], in0=z_of[j][e][:], scalar1=0.0)
                 else:
                     nc.scalar.activation(out=relu_of[j][:, e, :], in_=z_of[j][e][:], func=ACT.Relu)
 
         def square(j, on_vector):
-            tiles = tiles_of(j, on_vector)
+            tiles = tiles_of(j, on_vector, FIRST_SHARED_SQUARE)
             if not tiles:
                 return
             if tiles[0] == 0:
@@ -322,6 +327,10 @@ def tile_shepherdembryo_pb_t_kernel(tc, y_attn, x, w_o, attn_scale, w_fc, out_0,
         def run(stage, j, *arguments):
             if 0 <= j < N_GROUPS:
                 stage(j, *arguments)
+
+        def prepare_half_of_wfc(half):
+            transpose_weights("wfc", wfc_rows, half, "xn_T")
+            copy_weights_out("wfc", half, nc.scalar.copy)
 
         gather_heads(0)
         transpose_y(0)
@@ -344,9 +353,20 @@ def tile_shepherdembryo_pb_t_kernel(tc, y_attn, x, w_o, attn_scale, w_fc, out_0,
         gather_heads(1)
         transpose_y(1)
         copy_y_out(1, False)
-        copy_y_out(1, True)
 
-        for step in range(N_GROUPS + 4):
+        apply_gain(0)
+        copy_y_out(1, True)
+        gather_heads(2)
+        transpose_y(2)
+        quantise_y(1)
+        project_heads(1)
+        add_residual(0)
+        copy_y_out(2, False)
+        copy_y_out(2, True)
+        prepare_half_of_wfc(0)
+
+        for step in range(1, N_GROUPS + 4):
+            squares_last = step >= N_GROUPS
             for chunk in LOAD_STEP:
                 if LOAD_STEP[chunk] == step:
                     load_y(chunk)
@@ -358,8 +378,9 @@ def tile_shepherdembryo_pb_t_kernel(tc, y_attn, x, w_o, attn_scale, w_fc, out_0,
             run(apply_gain, step)
             run(project_up, step - 3)
             run(quantise_y, step + 1)
-            run(square, step - 4, False)
-            run(square, step - 4, True)
+            if not squares_last:
+                run(square, step - 4, False)
+                run(square, step - 4, True)
             run(invert_rms, step - 1)
             run(copy_xn_out, step - 2)
             run(project_heads, step + 1)
@@ -370,8 +391,10 @@ def tile_shepherdembryo_pb_t_kernel(tc, y_attn, x, w_o, attn_scale, w_fc, out_0,
             run(copy_y_out, step + 2, True)
             run(relu, step - 3, False)
             run(relu, step - 3, True)
-            if step < 2:
-                transpose_weights("wfc", wfc_rows, step, "xn_T")
-                copy_weights_out("wfc", step, nc.scalar.copy)
+            if squares_last:
+                run(square, step - 4, False)
+                run(square, step - 4, True)
+            if step == 1:
+                prepare_half_of_wfc(1)
             if step == 2:
                 quantise_weights("wfc")

@@ -26,8 +26,8 @@ GROUP = 2
 N_TILES = B * S // P
 N_GROUPS = N_TILES // GROUP
 TILES_OF_CHUNK = ((2, 2, 4, 4, 4), (8, 8))
-LOAD_STEP = {4: 1, 5: 2, 6: 6}
-MERGED_CHUNKS = (3, 4, 5, 6)
+LOAD_STEPS = {5: range(1, 5), 6: range(5, 9)}
+MERGED_CHUNKS = (5, 6)
 FIRST_SHARED_SQUARE = N_GROUPS - 6
 FIRST_SHARED_RELU = N_GROUPS - 4
 WARM_UP_MATMULS = 20
@@ -71,16 +71,24 @@ def tile_shepherdembryo_pb_t_kernel(tc, y_attn, x, w_o, attn_scale, w_fc, out_0,
         def load_y(chunk):
             b, first_token, tiles = chunks[chunk]
             tokens = y_attn[b, :, first_token : first_token + tiles * P, :]
-            if chunk in MERGED_CHUNKS:
-                y_chunk = const.tile([P, tiles, H, DH], BF16, name="y_chunk_%d" % chunk)
-                for head in range(H):
-                    nc.sync.dma_start(
-                        out=y_chunk[:, :, head, :], in_=tokens[head].rearrange("(p i) j -> p i j", i=tiles)
-                    )
-            else:
-                y_chunk = const.tile([P, H, tiles, DH], BF16, name="y_chunk_%d" % chunk)
-                nc.sync.dma_start(out=y_chunk[:], in_=tokens.rearrange("h (p i) j -> p h i j", i=tiles))
+            y_chunk = const.tile([P, H, tiles, DH], BF16, name="y_chunk_%d" % chunk)
+            nc.sync.dma_start(out=y_chunk[:], in_=tokens.rearrange("h (p i) j -> p h i j", i=tiles))
             y_chunks[chunk] = y_chunk
+
+        def load_part(chunk, part, parts):
+            b, first_token, tiles = chunks[chunk]
+            if part == 0:
+                y_chunk = const.tile([P, tiles, H, DH], BF16, name="y_chunk_%d" % chunk)
+                y_chunks[chunk] = y_chunk
+                x_chunk = const.tile([P, tiles, D], BF16, name="x_chunk_%d" % chunk)
+                x_chunks[chunk] = x_chunk
+            for head in range(part * H // parts, (part + 1) * H // parts):
+                tokens = y_attn[b, head, first_token : first_token + tiles * P, :]
+                nc.sync.dma_start(
+                    out=y_chunks[chunk][:, :, head, :], in_=tokens.rearrange("(p i) j -> p i j", i=tiles)
+                )
+            slots = slice(part * tiles // parts, (part + 1) * tiles // parts)
+            nc.sync.dma_start(out=x_chunks[chunk][:, slots, :], in_=token_rows(x, chunk)[:, slots, :])
 
         def load_x(chunk):
             x_chunk = const.tile([P, chunks[chunk][2], D], BF16, name="x_chunk_%d" % chunk)
@@ -181,7 +189,7 @@ def tile_shepherdembryo_pb_t_kernel(tc, y_attn, x, w_o, attn_scale, w_fc, out_0,
         def copy_y_out(j, on_vector):
             copy = nc.vector.tensor_copy if on_vector else nc.scalar.copy
             for e in range(GROUP):
-                if ((GROUP * j + e) % 3 == 2) == on_vector:
+                if ((GROUP * j + e) % 5 == 4) == on_vector:
                     copy(
                         out=y_grouped_of[j][:, e, :].bitcast(F32).rearrange("p (g r u) -> p g r u", g=PASSES_1, u=2),
                         in_=y_banks_of[j][e][:].rearrange("p (g u) r -> p g r u", u=2),
@@ -364,13 +372,15 @@ def tile_shepherdembryo_pb_t_kernel(tc, y_attn, x, w_o, attn_scale, w_fc, out_0,
         copy_y_out(2, False)
         copy_y_out(2, True)
         prepare_half_of_wfc(0)
+        load_y(4)
+        load_x(4)
 
         for step in range(1, N_GROUPS + 4):
             squares_last = step >= N_GROUPS
-            for chunk in LOAD_STEP:
-                if LOAD_STEP[chunk] == step:
-                    load_y(chunk)
-                    load_x(chunk)
+            for chunk in LOAD_STEPS:
+                steps = LOAD_STEPS[chunk]
+                if step in steps:
+                    load_part(chunk, step - steps.start, len(steps))
             run(transpose_xn, step - 2)
             run(sum_squares, step - 1)
             run(gather_heads, step + 2)

@@ -28,7 +28,7 @@ N_GROUPS = N_TILES // GROUP
 TILES_OF_CHUNK = ((2, 2, 4, 4, 4), (8, 8))
 LOAD_STEPS = {5: range(1, 5), 6: range(5, 9)}
 MERGED_CHUNKS = (5, 6)
-FIRST_SHARED_SQUARE = N_GROUPS - 6
+FIRST_SHARED_SQUARE = N_GROUPS - 5
 FIRST_SHARED_RELU = N_GROUPS - 4
 WARM_UP_MATMULS = 20
 
@@ -188,8 +188,9 @@ def tile_shepherdembryo_pb_t_kernel(tc, y_attn, x, w_o, attn_scale, w_fc, out_0,
 
         def copy_y_out(j, on_vector):
             copy = nc.vector.tensor_copy if on_vector else nc.scalar.copy
+            merged = place(j)[0] in MERGED_CHUNKS
             for e in range(GROUP):
-                if ((GROUP * j + e) % 5 == 4) == on_vector:
+                if (merged and e == GROUP - 1) == on_vector:
                     copy(
                         out=y_grouped_of[j][:, e, :].bitcast(F32).rearrange("p (g r u) -> p g r u", g=PASSES_1, u=2),
                         in_=y_banks_of[j][e][:].rearrange("p (g u) r -> p g r u", u=2),

@@ -26,8 +26,8 @@ GROUP = 2
 N_TILES = B * S // P
 N_GROUPS = N_TILES // GROUP
 TILES_OF_CHUNK = ((2, 2, 4, 4, 4), (8, 8))
-LOAD_STEPS = {5: range(1, 5), 6: range(5, 9)}
-MERGED_CHUNKS = (5, 6)
+LOAD_STEPS = {5: range(1, 4), 6: range(3, 7)}
+MERGED_CHUNKS = (3, 4, 5, 6)
 FIRST_SHARED_SQUARE = N_GROUPS - 5
 FIRST_SHARED_RELU = N_GROUPS - 4
 WARM_UP_MATMULS = 20
@@ -63,7 +63,7 @@ def tile_shepherdembryo_pb_t_kernel(tc, y_attn, x, w_o, attn_scale, w_fc, out_0,
         stack.enter_context(tc.manual_schedule())
         const = stack.enter_context(tc.tile_pool(name="const", bufs=1))
         work = stack.enter_context(tc.tile_pool(name="work", bufs=2))
-        results = stack.enter_context(tc.tile_pool(name="results", bufs=4))
+        results = stack.enter_context(tc.tile_pool(name="results", bufs=6))
         psum = stack.enter_context(tc.psum_pool(name="psum", bufs=2))
 
         y_chunks, x_chunks = {}, {}
@@ -115,8 +115,7 @@ def tile_shepherdembryo_pb_t_kernel(tc, y_attn, x, w_o, attn_scale, w_fc, out_0,
         nc.sync.dma_start(out=wfc_rows[:], in_=w_fc.rearrange("(a p) k -> p a k", p=P))
         load_x(1)
         load_x(2)
-        load_y(3)
-        load_x(3)
+        load_part(3, 0, 1)
 
         identity_f32 = const.tile([P, P], F32)
         make_identity(nc, identity_f32[:])
@@ -373,8 +372,7 @@ def tile_shepherdembryo_pb_t_kernel(tc, y_attn, x, w_o, attn_scale, w_fc, out_0,
         copy_y_out(2, False)
         copy_y_out(2, True)
         prepare_half_of_wfc(0)
-        load_y(4)
-        load_x(4)
+        load_part(4, 0, 1)
 
         for step in range(1, N_GROUPS + 4):
             squares_last = step >= N_GROUPS

@@ -27,7 +27,7 @@ N_TILES = B * S // P
 N_GROUPS = N_TILES // GROUP
 TILES_OF_CHUNK = ((2, 2, 4, 4, 4), (8, 8))
 LOAD_STEPS = {5: range(1, 4), 6: range(3, 7)}
-MERGED_CHUNKS = (3, 4, 5, 6)
+MERGED_CHUNKS = (5, 6)
 FIRST_SHARED_SQUARE = N_GROUPS - 5
 FIRST_SHARED_RELU = N_GROUPS - 4
 WARM_UP_MATMULS = 20
@@ -115,7 +115,8 @@ def tile_shepherdembryo_pb_t_kernel(tc, y_attn, x, w_o, attn_scale, w_fc, out_0,
         nc.sync.dma_start(out=wfc_rows[:], in_=w_fc.rearrange("(a p) k -> p a k", p=P))
         load_x(1)
         load_x(2)
-        load_part(3, 0, 1)
+        load_y(3)
+        load_x(3)
 
         identity_f32 = const.tile([P, P], F32)
         make_identity(nc, identity_f32[:])
@@ -234,9 +235,11 @@ def tile_shepherdembryo_pb_t_kernel(tc, y_attn, x, w_o, attn_scale, w_fc, out_0,
         def add_residual(j):
             chunk, slots = place(j)
             x_mid = results.tile([P, GROUP, D], F32)
-            nc.vector.tensor_tensor(
-                out=x_mid[:], in0=gained_of[j][:], in1=x_chunks[chunk][:, slots, :], op=ALU.add
-            )
+            residual = x_chunks[chunk][:, slots, :]
+            for part in [slice(e, e + 1) for e in range(GROUP)] if j == N_GROUPS - 1 else [slice(0, GROUP)]:
+                nc.vector.tensor_tensor(
+                    out=x_mid[:, part, :], in0=gained_of[j][:, part, :], in1=residual[:, part, :], op=ALU.add
+                )
             nc.sync.dma_start(out=token_rows(out_0, chunk)[:, slots, :], in_=x_mid[:])
             x_mid_of[j] = x_mid
 
@@ -244,9 +247,14 @@ def tile_shepherdembryo_pb_t_kernel(tc, y_attn, x, w_o, attn_scale, w_fc, out_0,
             sum_sq = work.tile([P, GROUP], F32)
             for e in range(GROUP):
                 squares = work.tile([P, D], F32)
-                nc.scalar.activation(
-                    out=squares[:], in_=x_mid_of[j][:, e, :], func=ACT.Square, accum_out=sum_sq[:, e : e + 1]
-                )
+                x_mid = x_mid_of[j][:, e, :]
+                total = sum_sq[:, e : e + 1]
+                if j == N_GROUPS - 1 and e == GROUP - 1:
+                    nc.vector.scalar_tensor_tensor(
+                        out=squares[:], in0=x_mid, scalar=1.0, in1=x_mid, op0=ALU.mult, op1=ALU.mult, accum_out=total
+                    )
+                else:
+                    nc.scalar.activation(out=squares[:], in_=x_mid, func=ACT.Square, accum_out=total)
             sum_sq_of[j] = sum_sq
 
         def invert_rms(j):
@@ -356,7 +364,7 @@ def tile_shepherdembryo_pb_t_kernel(tc, y_attn, x, w_o, attn_scale, w_fc, out_0,
         gain = const.tile([P, D], F32)
         gain_bank = psum.tile([P, D], F32, tag="attn")
         nc.tensor.matmul(out=gain_bank[:], lhsT=ones[:], rhs=gain_rows[:], start=True, stop=True)
-        nc.vector.tensor_copy(out=gain[:], in_=gain_bank[:])
+        nc.scalar.copy(out=gain[:], in_=gain_bank[:])
         project_heads(0)
         gather_heads(1)
         transpose_y(1)
@@ -372,7 +380,8 @@ def tile_shepherdembryo_pb_t_kernel(tc, y_attn, x, w_o, attn_scale, w_fc, out_0,
         copy_y_out(2, False)
         copy_y_out(2, True)
         prepare_half_of_wfc(0)
-        load_part(4, 0, 1)
+        load_y(4)
+        load_x(4)
 
         for step in range(1, N_GROUPS + 4):
             squares_last = step >= N_GROUPS

from contextlib import ExitStack

import concourse.mybir as mybir
from concourse.masks import make_identity

BF16 = mybir.dt.bfloat16
F32 = mybir.dt.float32
U32 = mybir.dt.uint32
U8 = mybir.dt.uint8
FP8X4 = mybir.dt.float8_e4m3fn_x4
ALU = mybir.AluOpType
ACT = mybir.ActivationFunctionType

P = 128
PACK = 4
K_PASS = P * PACK

B, H, S, DH = 2, 8, 2048, 128
E = H * DH
D = 512
F = 512
EPS = 1e-6

PASSES_1 = E // K_PASS
GROUP = 2
N_TILES = B * S // P
N_GROUPS = N_TILES // GROUP
TILES_OF_CHUNK = ((2, 2, 4, 4, 4), (8, 8))
LOAD_STEPS = {5: range(1, 4), 6: range(3, 7)}
MERGED_CHUNKS = (5, 6)
FIRST_SHARED_SQUARE = N_GROUPS - 5
FIRST_SHARED_RELU = N_GROUPS - 4
WARM_UP_MATMULS = 20

FLOPS = 2 * B * S * E * D + 2 * B * S * D * F


def transpose_pairs(nc, bank, rows, identity_f32):
    words = rows.bitcast(F32)
    for q in range(words.shape[1] // P):
        nc.tensor.transpose(bank[:, q, :], words[:, q * P : (q + 1) * P], identity_f32)


def tile_shepherdembryo_pb_t_kernel(tc, y_attn, x, w_o, attn_scale, w_fc, out_0, out_1):
    nc = tc.nc

    chunks = []
    chunk_of, slot_of = [], []
    for b, sizes in enumerate(TILES_OF_CHUNK):
        first_token = 0
        for tiles in sizes:
            chunk_of += [len(chunks)] * tiles
            slot_of += range(tiles)
            chunks.append((b, first_token, tiles))
            first_token += tiles * P

    def token_rows(dram, chunk):
        b, first_token, tiles = chunks[chunk]
        rows = dram[b, first_token : first_token + tiles * P, :]
        return rows.rearrange("(p i) d -> p i d", i=tiles)

    with ExitStack() as stack:
        stack.enter_context(tc.manual_schedule())
        const = stack.enter_context(tc.tile_pool(name="const", bufs=1))
        work = stack.enter_context(tc.tile_pool(name="work", bufs=2))
        results = stack.enter_context(tc.tile_pool(name="results", bufs=6))
        psum = stack.enter_context(tc.psum_pool(name="psum", bufs=2))

        y_chunks, x_chunks = {}, {}

        def load_y(chunk):
            b, first_token, tiles = chunks[chunk]
            tokens = y_attn[b, :, first_token : first_token + tiles * P, :]
            y_chunk = const.tile([P, H, tiles, DH], BF16, name="y_chunk_%d" % chunk)
            nc.sync.dma_start(out=y_chunk[:], in_=tokens.rearrange("h (p i) j -> p h i j", i=tiles))
            y_chunks[chunk] = y_chunk

        def load_part(chunk, part, parts):
            b, first_token, tiles = chunks[chunk]
            if part == 0:
                y_chunk = const.tile([P, tiles, H, DH], BF16, name="y_chunk_%d" % chunk)
                y_chunks[chunk] = y_chunk
                x_chunk = const.tile([P, tiles, D], BF16, name="x_chunk_%d" % chunk)
                x_chunks[chunk] = x_chunk
            for head in range(part * H // parts, (part + 1) * H // parts):
                tokens = y_attn[b, head, first_token : first_token + tiles * P, :]
                nc.sync.dma_start(
                    out=y_chunks[chunk][:, :, head, :], in_=tokens.rearrange("(p i) j -> p i j", i=tiles)
                )
            slots = slice(part * tiles // parts, (part + 1) * tiles // parts)
            nc.sync.dma_start(out=x_chunks[chunk][:, slots, :], in_=token_rows(x, chunk)[:, slots, :])

        def load_x(chunk):
            x_chunk = const.tile([P, chunks[chunk][2], D], BF16, name="x_chunk_%d" % chunk)
            nc.sync.dma_start(out=x_chunk[:], in_=token_rows(x, chunk))
            x_chunks[chunk] = x_chunk

        load_y(0)
        wo_rows = []
        for g in range(PASSES_1):
            wo_rows_g = const.tile([P, D // P, K_PASS], BF16, name="wo_rows_%d" % g)
            nc.sync.dma_start(
                out=wo_rows_g[:], in_=w_o[:, g * K_PASS : (g + 1) * K_PASS].rearrange("(a p) k -> p a k", p=P)
            )
            wo_rows.append(wo_rows_g)
        ones = const.tile([P, P], BF16)
        nc.vector.memset(ones[:], 1.0)
        gain_rows = const.tile([P, D], BF16)
        nc.vector.memset(gain_rows[:], 0.0)
        nc.sync.dma_start(out=gain_rows[0:1, :], in_=attn_scale.rearrange("(o d) -> o d", o=1))
        load_y(1)
        load_x(0)
        load_y(2)
        wfc_rows = const.tile([P, F // P, D], BF16)
        nc.sync.dma_start(out=wfc_rows[:], in_=w_fc.rearrange("(a p) k -> p a k", p=P))
        load_x(1)
        load_x(2)
        load_y(3)
        load_x(3)

        identity_f32 = const.tile([P, P], F32)
        make_identity(nc, identity_f32[:])
        eps = const.tile([P, 1], F32)
        nc.vector.memset(eps[:], EPS)
        warm_up_bank = psum.tile([P, P], F32, tag="attn")
        for repeat in range(WARM_UP_MATMULS):
            nc.tensor.matmul(out=warm_up_bank[:], lhsT=ones[:], rhs=ones[:], start=True, stop=True)
        table_loader = const.tile([P, 1], F32)
        nc.scalar.activation(out=table_loader[:], in_=eps[:], func=ACT.Abs_reciprocal_sqrt)

        weight_banks = {}

        def transpose_weights(name, rows, half, tag):
            bank = psum.tile([P, PACK, P], F32, tag=tag, name="%s_%d_T" % (name, half))
            for a in range(2):
                transpose_pairs(nc, bank[:, 2 * a : 2 * a + 2, :], rows[:, 2 * half + a, :], identity_f32[:])
            weight_banks[name, half] = bank

        grouped_weights = {}

        def copy_weights_out(name, half, copy):
            if half == 0:
                grouped = const.tile([P, D * PACK], BF16, align_bytes=64, name=name + "_grouped")
                grouped_weights[name] = grouped
            words = grouped_weights[name][:].bitcast(F32).rearrange("p (a r u) -> p a r u", a=D // P, u=2)
            copy(
                out=words[:, 2 * half : 2 * half + 2, :, :],
                in_=weight_banks[name, half][:].rearrange("p (a u) r -> p a r u", u=2),
            )

        quantised_weights = {}

        def quantise_weights(name):
            codes = const.tile([P, D], U32, align_bytes=64, name=name + "_codes")
            scales = const.tile([P, D], U8, align_bytes=64, name=name + "_scales")
            nc.vector.quantize_mx(out=codes[:].bitcast(FP8X4), scales=scales[:], in_=grouped_weights[name][:])
            quantised_weights[name] = (codes, scales)

        y_rows_of, y_banks_of, y_grouped_of, y_quantised_of, attn_of = {}, {}, {}, {}, {}
        gained_of, x_mid_of, sum_sq_of, inv_rms_of = {}, {}, {}, {}
        xn_of, xn_bank_of, xn_grouped_of, xn_quantised_of, z_of, relu_of, h_of = {}, {}, {}, {}, {}, {}, {}

        def place(j):
            first = slot_of[GROUP * j]
            return chunk_of[GROUP * j], slice(first, first + GROUP)

        def gather_heads(j):
            chunk, slots = place(j)
            if chunk in MERGED_CHUNKS:
                y_rows_of[j] = y_chunks[chunk][:, slots, :, :].rearrange("p i h j -> p i (h j)")
                return
            y_rows = work.tile([P, GROUP, E], BF16)
            nc.vector.tensor_copy(
                out=y_rows[:].rearrange("p i (h j) -> p i h j", h=H),
                in_=y_chunks[chunk][:, :, slots, :].rearrange("p h i j -> p i h j"),
            )
            y_rows_of[j] = y_rows[:]

        def transpose_y(j):
            banks = []
            for e in range(GROUP):
                y_T = psum.tile([P, 2 * PASSES_1, P], F32)
                transpose_pairs(nc, y_T, y_rows_of[j][:, e, :], identity_f32[:])
                banks.append(y_T)
            y_banks_of[j] = banks
            y_grouped = work.tile([P, GROUP, E], BF16, align_bytes=64)
            y_grouped_of[j] = y_grouped

        def copy_y_out(j, on_vector):
            copy = nc.vector.tensor_copy if on_vector else nc.scalar.copy
            merged = place(j)[0] in MERGED_CHUNKS
            for e in range(GROUP):
                if (merged and e == GROUP - 1) == on_vector:
                    copy(
                        out=y_grouped_of[j][:, e, :].bitcast(F32).rearrange("p (g r u) -> p g r u", g=PASSES_1, u=2),
                        in_=y_banks_of[j][e][:].rearrange("p (g u) r -> p g r u", u=2),
                    )

        def quantise_y(j):
            y_codes = work.tile([P, GROUP * PASSES_1 * P], U32, align_bytes=64)
            y_scales = work.tile([P, GROUP * PASSES_1 * P], U8, align_bytes=64)
            nc.vector.quantize_mx(
                out=y_codes[:].bitcast(FP8X4),
                scales=y_scales[:],
                in_=y_grouped_of[j][:].rearrange("p i k -> p (i k)"),
            )
            y_quantised_of[j] = (y_codes, y_scales)

        def project_heads(j):
            y_codes, y_scales = y_quantised_of[j]
            banks = []
            for e in range(GROUP):
                attn = psum.tile([P, D], F32)
                for g in range(PASSES_1):
                    wo_codes, wo_scales = quantised_weights["wo_%d" % g]
                    columns = slice((e * PASSES_1 + g) * P, (e * PASSES_1 + g + 1) * P)
                    nc.tensor.matmul_mx(
                        out=attn[:],
                        lhsT=y_codes[:, columns].bitcast(FP8X4),
                        lhsT_scale=y_scales[:, columns],
                        rhs=wo_codes[:].bitcast(FP8X4),
                        rhs_scale=wo_scales[:],
                        start=(g == 0),
                        stop=(g == PASSES_1 - 1),
                    )
                banks.append(attn)
            attn_of[j] = banks

        def apply_gain(j):
            gained = work.tile([P, GROUP, D], F32)
            for e in range(GROUP):
                nc.vector.tensor_tensor(out=gained[:, e, :], in0=attn_of[j][e][:], in1=gain[:], op=ALU.mult)
            gained_of[j] = gained

        def add_residual(j):
            chunk, slots = place(j)
            x_mid = results.tile([P, GROUP, D], F32)
            residual = x_chunks[chunk][:, slots, :]
            for part in [slice(e, e + 1) for e in range(GROUP)] if j == N_GROUPS - 1 else [slice(0, GROUP)]:
                nc.vector.tensor_tensor(
                    out=x_mid[:, part, :], in0=gained_of[j][:, part, :], in1=residual[:, part, :], op=ALU.add
                )
            nc.sync.dma_start(out=token_rows(out_0, chunk)[:, slots, :], in_=x_mid[:])
            x_mid_of[j] = x_mid

        def sum_squares(j):
            sum_sq = work.tile([P, GROUP], F32)
            for e in range(GROUP):
                squares = work.tile([P, D], F32)
                x_mid = x_mid_of[j][:, e, :]
                total = sum_sq[:, e : e + 1]
                if j == N_GROUPS - 1 and e == GROUP - 1:
                    nc.vector.scalar_tensor_tensor(
                        out=squares[:], in0=x_mid, scalar=1.0, in1=x_mid, op0=ALU.mult, op1=ALU.mult, accum_out=total
                    )
                else:
                    nc.scalar.activation(out=squares[:], in_=x_mid, func=ACT.Square, accum_out=total)
            sum_sq_of[j] = sum_sq

        def invert_rms(j):
            inv_rms = work.tile([P, GROUP], F32)
            nc.scalar.activation(
                out=inv_rms[:], in_=sum_sq_of[j][:], func=ACT.Abs_reciprocal_sqrt, bias=eps[:], scale=1.0 / D
            )
            inv_rms_of[j] = inv_rms

        def normalise(j):
            xn = work.tile([P, GROUP, D], BF16)
            for e in range(GROUP):
                nc.vector.tensor_scalar_mul(
                    out=xn[:, e, :], in0=x_mid_of[j][:, e, :], scalar1=inv_rms_of[j][:, e : e + 1]
                )
            xn_of[j] = xn

        def transpose_xn(j):
            xn_T = psum.tile([P, PACK, P], F32)
            for e in range(GROUP):
                transpose_pairs(nc, xn_T[:, 2 * e : 2 * e + 2, :], xn_of[j][:, e, :], identity_f32[:])
            xn_bank_of[j] = xn_T

        def copy_xn_out(j):
            xn_grouped = work.tile([P, GROUP * D], BF16, align_bytes=64)
            nc.scalar.copy(
                out=xn_grouped[:].bitcast(F32).rearrange("p (i r u) -> p i r u", i=GROUP, u=2),
                in_=xn_bank_of[j][:].rearrange("p (i u) r -> p i r u", u=2),
            )
            xn_grouped_of[j] = xn_grouped

        def quantise_xn(j):
            xn_codes = work.tile([P, GROUP * P], U32, align_bytes=64)
            xn_scales = work.tile([P, GROUP * P], U8, align_bytes=64)
            nc.vector.quantize_mx(out=xn_codes[:].bitcast(FP8X4), scales=xn_scales[:], in_=xn_grouped_of[j][:])
            xn_quantised_of[j] = (xn_codes, xn_scales)

        def project_up(j):
            xn_codes, xn_scales = xn_quantised_of[j]
            wfc_codes, wfc_scales = quantised_weights["wfc"]
            banks = []
            for e in range(GROUP):
                z = psum.tile([P, F], F32)
                nc.tensor.matmul_mx(
                    out=z[:],
                    lhsT=xn_codes[:, e * P : (e + 1) * P].bitcast(FP8X4),
                    lhsT_scale=xn_scales[:, e * P : (e + 1) * P],
                    rhs=wfc_codes[:].bitcast(FP8X4),
                    rhs_scale=wfc_scales[:],
                    start=True,
                    stop=True,
                )
                banks.append(z)
            z_of[j] = banks
            positive = work.tile([P, GROUP, F], F32)
            relu_of[j] = positive

        def tiles_of(j, on_vector, first_shared_group):
            return [e for e in range(GROUP) if (j >= first_shared_group and e == GROUP - 1) == on_vector]

        def relu(j, on_vector):
            for e in tiles_of(j, on_vector, FIRST_SHARED_RELU):
                if on_vector:
                    nc.vector.tensor_scalar_max(out=relu_of[j][:, e, :], in0=z_of[j][e][:], scalar1=0.0)
                else:
                    nc.scalar.activation(out=relu_of[j][:, e, :], in_=z_of[j][e][:], func=ACT.Relu)

        def square(j, on_vector):
            tiles = tiles_of(j, on_vector, FIRST_SHARED_SQUARE)
            if not tiles:
                return
            if tiles[0] == 0:
                h = results.tile([P, GROUP, F], F32)
                h_of[j] = h
            part = slice(tiles[0], tiles[-1] + 1)
            positive = relu_of[j][:, part, :]
            squared = h_of[j][:, part, :]
            if on_vector:
                nc.vector.tensor_tensor(out=squared, in0=positive, in1=positive, op=ALU.mult)
            else:
                nc.scalar.activation(out=squared, in_=positive, func=ACT.Square)
            chunk, slots = place(j)
            rows = token_rows(out_1, chunk)[:, slots, :]
            nc.sync.dma_start(out=rows[:, part, :], in_=squared)

        def run(stage, j, *arguments):
            if 0 <= j < N_GROUPS:
                stage(j, *arguments)

        def prepare_half_of_wfc(half):
            transpose_weights("wfc", wfc_rows, half, "xn_T")
            copy_weights_out("wfc", half, nc.scalar.copy)

        gather_heads(0)
        transpose_y(0)
        for half in range(2):
            transpose_weights("wo_0", wo_rows[0], half, "z")
        for half in range(2):
            transpose_weights("wo_1", wo_rows[1], half, "xn_T")
        copy_y_out(0, False)
        for half in range(2):
            copy_weights_out("wo_0", half, nc.vector.tensor_copy)
            copy_weights_out("wo_1", half, nc.scalar.copy)
        quantise_y(0)
        quantise_weights("wo_0")
        quantise_weights("wo_1")
        gain = const.tile([P, D], F32)
        gain_bank = psum.tile([P, D], F32, tag="attn")
        nc.tensor.matmul(out=gain_bank[:], lhsT=ones[:], rhs=gain_rows[:], start=True, stop=True)
        nc.scalar.copy(out=gain[:], in_=gain_bank[:])
        project_heads(0)
        gather_heads(1)
        transpose_y(1)
        copy_y_out(1, False)

        apply_gain(0)
        copy_y_out(1, True)
        gather_heads(2)
        transpose_y(2)
        quantise_y(1)
        project_heads(1)
        add_residual(0)
        copy_y_out(2, False)
        copy_y_out(2, True)
        prepare_half_of_wfc(0)
        load_y(4)
        load_x(4)

        for step in range(1, N_GROUPS + 4):
            squares_last = step >= N_GROUPS
            for chunk in LOAD_STEPS:
                steps = LOAD_STEPS[chunk]
                if step in steps:
                    load_part(chunk, step - steps.start, len(steps))
            run(transpose_xn, step - 2)
            run(sum_squares, step - 1)
            run(gather_heads, step + 2)
            run(transpose_y, step + 2)
            run(apply_gain, step)
            run(project_up, step - 3)
            run(quantise_y, step + 1)
            if not squares_last:
                run(square, step - 4, False)
                run(square, step - 4, True)
            run(invert_rms, step - 1)
            run(copy_xn_out, step - 2)
            run(project_heads, step + 1)
            run(add_residual, step)
            run(copy_y_out, step + 2, False)
            run(normalise, step - 1)
            run(quantise_xn, step - 2)
            run(copy_y_out, step + 2, True)
            run(relu, step - 3, False)
            run(relu, step - 3, True)
            if squares_last:
                run(square, step - 4, False)
                run(square, step - 4, True)
            if step == 1:
                prepare_half_of_wfc(1)
            if step == 2:
                quantise_weights("wfc")
